import numpy as np
import ml_dtypes


def mxq(x, axis, fmt="e4m3"):
    dtype, down = {"e4m3": (ml_dtypes.float8_e4m3fn, 7), "e5m2": (ml_dtypes.float8_e5m2, 14)}[fmt]
    v = np.moveaxis(np.asarray(x, np.float32).astype(ml_dtypes.bfloat16).astype(np.float64), axis, -1)
    blocks = v.reshape(v.shape[:-1] + (-1, 32))
    amax = np.abs(blocks).max(-1, keepdims=True)
    byte = np.maximum(np.where(amax > 0, np.frexp(amax)[1] - 1 + 127, 0) - down, 1)
    scale = np.exp2(byte - 127.0)
    codes = (blocks / scale).astype(np.float32).astype(dtype).astype(np.float64)
    return np.moveaxis((codes * scale).reshape(v.shape), -1, axis)


WIDE = False


def mx_kscale(k):
    if not WIDE:
        return np.ones(k)
    levels = np.array([10, -10, 5, -5, 0])
    a = np.random.permutation(np.resize(levels, k // 512 * 4)).reshape(k // 512, 4)
    idx = np.arange(k)
    return np.exp2(a[idx // 512, idx % 128 // 32])


BF16 = ml_dtypes.bfloat16


def bf(x):
    return np.asarray(x, np.float32).astype(BF16)


def f64(x):
    return np.asarray(x).astype(np.float64)


E2M1 = np.array([0.0, 0.5, 1.0, 1.5, 2.0, 3.0, 4.0, 6.0, -0.0, -0.5, -1.0, -1.5, -2.0, -3.0, -4.0, -6.0])


def pack_weight(w, fmt):
    k, n = w.shape
    w = f64(bf(w)).reshape(k // 32, 32, n)
    amax = np.abs(w).max(1)
    if fmt == "e4m3":
        byte = np.frexp(amax)[1] - 1 + 127 - 7
    else:
        mant, ex = np.frexp(amax / 6.0)
        byte = np.where(mant > 0.5, ex, ex - 1) + 127
    byte = np.clip(np.where(amax > 0, byte, 1), 1, 254)
    scaled = (w * np.exp2(127.0 - byte)[:, None, :]).reshape(k, n).astype(np.float32)
    by_word = np.ascontiguousarray(scaled.reshape(k // 512, 128, 4, n).transpose(0, 1, 3, 2))
    if fmt == "e4m3":
        words = by_word.astype(ml_dtypes.float8_e4m3fn).view(np.uint8)
    else:
        c = by_word.astype(ml_dtypes.float4_e2m1fn).view(np.uint8) & 0xF
        words = c[..., 0::2] | (c[..., 1::2] << 4)
    return np.ascontiguousarray(words), np.ascontiguousarray(byte.astype(np.uint8).reshape(k // 512, 16, n))


def unpack_weight(words, scales, fmt):
    g, p, n, _ = words.shape
    if fmt == "e4m3":
        vals = np.ascontiguousarray(words).view(ml_dtypes.float8_e4m3fn).astype(np.float64)
    else:
        nib = np.empty((g, p, n, 4), np.uint8)
        nib[..., 0::2] = words & 0xF
        nib[..., 1::2] = words >> 4
        vals = E2M1[nib]
    vals = vals * np.repeat(np.exp2(scales.astype(np.float64) - 127.0), 8, axis=1)[..., None]
    return vals.transpose(0, 1, 3, 2).reshape(g * 512, n)


B, T, D, O = 8, 32, 16384, 1024


def erf(z):
    a = np.clip(z, -6.0, 6.0)
    q = 2.0 * a * a
    term = a.copy()
    total = a.copy()
    for k in range(1, 130):
        term = term * q / (2 * k + 1)
        total = total + term
    return 2.0 / np.sqrt(np.pi) * np.exp(-a * a) * total


def gelu_exact(v):
    return 0.5 * v * (1.0 + erf(v / np.sqrt(2.0)))


def setup_inputs():
    s = mx_kscale(D)
    x = np.random.standard_normal((B, T, D)) * s
    lengths = np.random.randint(T // 4, T + 1, size=B)
    lengths[np.random.randint(B)] = T
    pad = np.arange(T)[None, :] >= lengths[:, None]
    x = np.where(pad[:, :, None], -1.0, x)
    w = np.random.standard_normal((O, D)) / np.sqrt(D) / s[None, :]
    words, scales = pack_weight(np.ascontiguousarray(w.T), "e4m3")
    return {"x": bf(x), "W_words": words, "W_scales": scales, "b": bf(np.random.standard_normal(O) * 0.3)}


def reference(x, W_words, W_scales, b):
    x = f64(x)
    valid = ~np.all(x == -1.0, axis=-1)
    y = gelu_exact((mxq(x, 2, "e4m3") @ unpack_weight(W_words, W_scales, "e4m3")) + f64(b))
    vf = valid[..., None].astype(np.float64)
    n = np.sum(vf, axis=1)
    mean = np.sum(y * vf, axis=1) / n
    diff = (y - mean[:, None, :]) * vf
    var = np.sum(diff * diff, axis=1) / np.maximum(n - 1.0, 1.0)
    std = np.where(n > 1.0, np.sqrt(var), np.zeros_like(var))
    out = np.concatenate([std, mean], axis=-1)
    return np.where(np.isnan(out), np.zeros_like(out), out)

@@ -1,0 +1,256 @@
+from contextlib import ExitStack
+
+import concourse.mybir as mybir
+from concourse.masks import make_identity
+
+F32 = mybir.dt.float32
+BF16 = mybir.dt.bfloat16
+I32 = mybir.dt.int32
+U32 = mybir.dt.uint32
+U8 = mybir.dt.uint8
+FP8X4 = mybir.dt.float8_e4m3fn_x4
+ALU = mybir.AluOpType
+ACT = mybir.ActivationFunctionType
+AXIS = mybir.AxisListType
+
+P = 128
+PACK = 4
+K_PASS = P * PACK
+WORDS_PASS = K_PASS // 2
+BANKS = 8
+
+SAMPLES = 8
+SAMPLE_TOKENS = 32
+TOKENS = SAMPLES * SAMPLE_TOKENS
+TOKEN_TILES = TOKENS // P
+FEATURES = 16384
+OUTPUTS = 1024
+PASSES = FEATURES // K_PASS
+OUT_TILES = OUTPUTS // P
+
+X_CHUNK = 4
+X_CHUNKS = PASSES // X_CHUNK
+PAIR = 2
+PLANES = 4
+assert X_CHUNK == PLANES
+W_CHUNK = 2
+W_BUFS = 8
+LATE_PASSES = 12
+GROUP_TILES = 2
+SMALLEST_VARIANCE_SUM = 1e-30
+
+FLOPS = 2 * TOKENS * FEATURES * OUTPUTS
+
+
+def tile_linearnnencoder_k_kernel(tc, x, W_words, W_scales, b, out):
+    nc = tc.nc
+    with ExitStack() as stack:
+        stack.enter_context(tc.manual_schedule())
+        keep = stack.enter_context(tc.tile_pool(name="keep", bufs=1))
+        stage = stack.enter_context(tc.tile_pool(name="stage", bufs=4))
+        w_pool = stack.enter_context(tc.tile_pool(name="w_pool", bufs=W_BUFS))
+        y_pool = stack.enter_context(tc.tile_pool(name="y_pool", bufs=4))
+        psum = stack.enter_context(tc.psum_pool(name="psum", bufs=1))
+
+        ident = keep.tile([P, P], F32)
+        make_identity(nc, ident[:])
+
+        w_planes = keep.tile([P, PASSES // PLANES, OUTPUTS], U8, align_bytes=64)
+        nc.vector.memset(w_planes[:].bitcast(I32), 0)
+
+        warm = keep.tile([P, 1], F32)
+        nc.vector.memset(warm[:], 0.0)
+        nc.scalar.activation(out=warm[:], in_=warm[:], func=ACT.Gelu)
+
+        b_rows = keep.tile([OUT_TILES, P], BF16)
+        nc.sync.dma_start(out=b_rows[:], in_=b.rearrange("(j n) -> j n", n=P))
+        b_square = keep.tile([P, P], F32)
+        nc.vector.memset(b_square[:], 0.0)
+        nc.vector.tensor_copy(out=b_square[0:OUT_TILES, :], in_=b_rows[:])
+        b_bank = psum.tile([P, P], F32, tag="bank7")
+        nc.tensor.transpose(b_bank[:], b_square[:], ident[:])
+        b_col = keep.tile([P, OUT_TILES], F32)
+        nc.vector.tensor_copy(out=b_col[:], in_=b_bank[:, 0:OUT_TILES])
+
+        x_view = x.flatten_outer_dims().rearrange("(h p) k -> p h k", p=P)
+        x_cols = X_CHUNK * K_PASS
+        x_tiles = []
+        for c in range(X_CHUNKS):
+            x_tile = keep.tile([P, TOKEN_TILES, x_cols], BF16, name="x%d" % c)
+            nc.sync.dma_start(out=x_tile[:], in_=x_view[:, :, c * x_cols : (c + 1) * x_cols])
+            x_tiles.append(x_tile)
+            for quad in range(4):
+                nc.sync.dma_start(
+                    out=w_planes[32 * quad : 32 * quad + 4 * PLANES, c, :].bitcast(I32),
+                    in_=W_scales[PLANES * c : PLANES * (c + 1), 4 * quad : 4 * quad + 4, :].bitcast(I32),
+                )
+
+        x_codes = keep.tile([P, PASSES * TOKENS], U32, align_bytes=64)
+        x_scales = keep.tile([P, PASSES * TOKENS], U8, align_bytes=64)
+
+        def transpose_pass(g, grouped_pass):
+            first_word = (g % X_CHUNK) * WORDS_PASS
+            bank = psum.tile([P, 2, TOKENS], F32, tag="bank%d" % (g % BANKS), name="x_bank")
+            for h in range(TOKEN_TILES):
+                words = x_tiles[g // X_CHUNK][:, h, :].bitcast(F32)
+                for u in range(2):
+                    nc.tensor.transpose(
+                        bank[:, u, h * P : (h + 1) * P],
+                        words[:, first_word + u : first_word + WORDS_PASS : 2],
+                        ident[:],
+                    )
+            copy = nc.vector.tensor_copy if g % 4 == 3 else nc.scalar.copy
+            copy(out=grouped_pass.bitcast(F32), in_=bank[:].rearrange("p u r -> p r u"))
+
+        def quantise_pair(q, grouped):
+            cols = slice(q * PAIR * TOKENS, (q + 1) * PAIR * TOKENS)
+            nc.vector.quantize_mx(
+                out=x_codes[:, cols].bitcast(FP8X4),
+                scales=x_scales[:, cols],
+                in_=grouped[:].rearrange("p g r t -> p (g r t)"),
+            )
+
+        copied = None
+        for q in range(PASSES // PAIR):
+            grouped = stage.tile([P, PAIR, TOKENS, PACK], BF16, align_bytes=64)
+            for i in range(PAIR):
+                transpose_pass(PAIR * q + i, grouped[:, i])
+            if copied is not None:
+                quantise_pair(q - 1, copied)
+            copied = grouped
+        quantise_pair(PASSES // PAIR - 1, copied)
+
+        differs = keep.tile([P, TOKEN_TILES, X_CHUNKS], F32)
+        for c in range(X_CHUNKS):
+            for h in range(TOKEN_TILES):
+                nc.vector.tensor_scalar(
+                    out=x_tiles[c][:, h, :],
+                    in0=x_tiles[c][:, h, :],
+                    scalar1=-1.0,
+                    scalar2=None,
+                    op0=ALU.not_equal,
+                    op1=ALU.max,
+                    accum_out=differs[:, h, c : c + 1],
+                )
+        valid = keep.tile([P, TOKEN_TILES], F32)
+        nc.vector.tensor_reduce(out=valid[:], in_=differs[:], axis=AXIS.X, op=ALU.max)
+
+        acc = [psum.tile([P, TOKENS], F32, tag="bank%d" % j, name="acc%d" % j) for j in range(OUT_TILES)]
+
+        def multiply(first_pass, first_tile, tiles):
+            w_tile = w_pool.tile([P, W_CHUNK, tiles * P], U32, tag="w%d" % tiles, align_bytes=64)
+            columns = slice(first_tile * P, (first_tile + tiles) * P)
+            nc.sync.dma_start(
+                out=w_tile[:].bitcast(I32),
+                in_=W_words[first_pass : first_pass + W_CHUNK, :, columns, :]
+                .rearrange("g p n t -> p g (n t)")
+                .bitcast(I32),
+            )
+            for i in range(W_CHUNK):
+                g = first_pass + i
+                for jj in range(tiles):
+                    j = first_tile + jj
+                    nc.tensor.matmul_mx(
+                        out=acc[j][:],
+                        lhsT=w_tile[:, i, jj * P : (jj + 1) * P].bitcast(FP8X4),
+                        lhsT_scale=w_planes[4 * (g % PLANES) : P, g // PLANES, j * P : (j + 1) * P],
+                        rhs=x_codes[:, g * TOKENS : (g + 1) * TOKENS].bitcast(FP8X4),
+                        rhs_scale=x_scales[:, g * TOKENS : (g + 1) * TOKENS],
+                        start=(g == 0),
+                        stop=(g == PASSES - 1),
+                    )
+
+        results = keep.tile([P, SAMPLES, 2, OUT_TILES], F32)
+        variance = keep.tile([P, SAMPLES, OUT_TILES], F32)
+        mask = keep.tile([P, TOKENS], F32)
+        inv_n = keep.tile([P, SAMPLES], F32)
+        inv_n1 = keep.tile([P, SAMPLES], F32)
+
+        def make_mask():
+            mask_bank = psum.tile([P, TOKENS], F32, tag="bank0")
+            for h in range(TOKEN_TILES):
+                nc.tensor.matmul(
+                    out=mask_bank[:, h * P : (h + 1) * P],
+                    lhsT=valid[:, h : h + 1].to_broadcast([P, P]),
+                    rhs=ident[:],
+                    start=True,
+                    stop=True,
+                )
+            nc.vector.tensor_copy(out=mask[:], in_=mask_bank[:])
+            count = keep.tile([P, SAMPLES], F32)
+            nc.vector.tensor_reduce(out=count[:], in_=by_sample(mask), axis=AXIS.X, op=ALU.add)
+            nc.vector.tensor_scalar_max(out=inv_n[:], in0=count[:], scalar1=1.0)
+            nc.vector.reciprocal(out=inv_n[:], in_=inv_n[:])
+            nc.vector.tensor_scalar(
+                out=inv_n1[:], in0=count[:], scalar1=-1.0, scalar2=1.0, op0=ALU.add, op1=ALU.max
+            )
+            nc.vector.reciprocal(out=inv_n1[:], in_=inv_n1[:])
+
+        def by_sample(row):
+            return row[:].rearrange("p (s t) -> p s t", t=SAMPLE_TOKENS)
+
+        def gelu(group):
+            ys = []
+            for j in group:
+                y = y_pool.tile([P, TOKENS], F32)
+                nc.scalar.activation(out=y[:], in_=acc[j][:], func=ACT.Gelu, bias=b_col[:, j : j + 1], scale=1.0)
+                ys.append((j, y))
+            return ys
+
+        def statistics(ys):
+            for j, y in ys:
+                nc.vector.tensor_tensor(out=y[:], in0=y[:], in1=mask[:], op=ALU.mult)
+            for j, y in ys:
+                total = y_pool.tile([P, SAMPLES], F32)
+                nc.vector.tensor_reduce(out=total[:], in_=by_sample(y), axis=AXIS.X, op=ALU.add)
+                nc.vector.tensor_tensor(out=results[:, :, 1, j], in0=total[:], in1=inv_n[:], op=ALU.mult)
+            for j, y in ys:
+                nc.vector.tensor_tensor(
+                    out=by_sample(y),
+                    in0=by_sample(y),
+                    in1=results[:, :, 1, j].unsqueeze(2).to_broadcast([P, SAMPLES, SAMPLE_TOKENS]),
+                    op=ALU.subtract,
+                )
+            for j, y in ys:
+                nc.vector.tensor_tensor(out=y[:], in0=y[:], in1=mask[:], op=ALU.mult)
+                nc.scalar.activation(out=y[:], in_=y[:], func=ACT.Square)
+            for j, y in ys:
+                squares = y_pool.tile([P, SAMPLES], F32)
+                nc.vector.tensor_reduce(out=squares[:], in_=by_sample(y), axis=AXIS.X, op=ALU.add)
+                nc.vector.scalar_tensor_tensor(
+                    out=variance[:, :, j],
+                    in0=squares[:],
+                    scalar=SMALLEST_VARIANCE_SUM,
+                    in1=inv_n1[:],
+                    op0=ALU.max,
+                    op1=ALU.mult,
+                )
+
+        def root(first_tile, tiles):
+            cols = slice(first_tile, first_tile + tiles)
+            nc.scalar.activation(out=results[:, :, 0, cols], in_=variance[:, :, cols], func=ACT.Sqrt)
+
+        early = PASSES - LATE_PASSES
+        for first_pass in range(0, early, W_CHUNK):
+            multiply(first_pass, 0, OUT_TILES)
+        last_group = OUT_TILES - GROUP_TILES
+        for first_tile in range(0, OUT_TILES, GROUP_TILES):
+            for first_pass in range(early, PASSES, W_CHUNK):
+                multiply(first_pass, first_tile, GROUP_TILES)
+            ys = gelu(range(first_tile, first_tile + GROUP_TILES))
+            if first_tile == 0:
+                make_mask()
+            if first_tile == last_group:
+                root(0, last_group)
+            statistics(ys)
+        root(last_group, GROUP_TILES)
+
+        out_bank = psum.tile([P, P], F32, tag="bank1")
+        nc.tensor.transpose(out_bank[:], results[:].rearrange("p s i j -> p (s i j)"), ident[:])
+        positive = keep.tile([P, P], F32)
+        nc.vector.tensor_scalar_max(out=positive[:], in0=out_bank[:], scalar1=0.0)
+        final = keep.tile([P, P], F32)
+        nc.vector.scalar_tensor_tensor(
+            out=final[:], in0=out_bank[:], scalar=0.0, in1=positive[:], op0=ALU.min, op1=ALU.add
+        )
+        nc.sync.dma_start(out=out.rearrange("s (c n) -> (s c) n", n=P), in_=final[:])

@@ -120,20 +120,31 @@ def tile_linearnnencoder_k_kernel(tc, x, W_words, W_scales, b, out):
             copied = grouped
         quantise_pair(PASSES // PAIR - 1, copied)
 
-        differs = keep.tile([P, TOKEN_TILES, X_CHUNKS], F32)
+        differs = keep.tile([P, X_CHUNKS], F32)
+        distance = keep.tile([P, X_CHUNKS], F32)
         for c in range(X_CHUNKS):
-            for h in range(TOKEN_TILES):
-                nc.vector.tensor_scalar(
-                    out=x_tiles[c][:, h, :],
-                    in0=x_tiles[c][:, h, :],
-                    scalar1=-1.0,
-                    scalar2=None,
-                    op0=ALU.not_equal,
-                    op1=ALU.max,
-                    accum_out=differs[:, h, c : c + 1],
-                )
+            nc.vector.tensor_scalar(
+                out=x_tiles[c][:, 0, :],
+                in0=x_tiles[c][:, 0, :],
+                scalar1=-1.0,
+                scalar2=None,
+                op0=ALU.not_equal,
+                op1=ALU.max,
+                accum_out=differs[:, c : c + 1],
+            )
+            nc.scalar.activation(
+                out=x_tiles[c][:, 1, :],
+                in_=x_tiles[c][:, 1, :],
+                func=ACT.Square,
+                bias=1.0,
+                scale=1.0,
+                accum_out=distance[:, c : c + 1],
+            )
         valid = keep.tile([P, TOKEN_TILES], F32)
-        nc.vector.tensor_reduce(out=valid[:], in_=differs[:], axis=AXIS.X, op=ALU.max)
+        row_distance = keep.tile([P, 1], F32)
+        nc.vector.tensor_reduce(out=valid[:, 0:1], in_=differs[:], axis=AXIS.X, op=ALU.max)
+        nc.vector.tensor_reduce(out=row_distance[:], in_=distance[:], axis=AXIS.X, op=ALU.add)
+        nc.vector.tensor_single_scalar(out=valid[:, 1:2], in_=row_distance[:], scalar=0.0, op=ALU.not_equal)
 
         acc = [psum.tile([P, TOKENS], F32, tag="bank%d" % j, name="acc%d" % j) for j in range(OUT_TILES)]
 

@@ -32,7 +32,6 @@ X_CHUNK = 4
 X_CHUNKS = PASSES // X_CHUNK
 PAIR = 2
 PLANES = 4
-assert X_CHUNK == PLANES
 W_CHUNK = 2
 W_BUFS = 8
 LATE_PASSES = 12
@@ -79,10 +78,12 @@ def tile_linearnnencoder_k_kernel(tc, x, W_words, W_scales, b, out):
             x_tile = keep.tile([P, TOKEN_TILES, x_cols], BF16, name="x%d" % c)
             nc.sync.dma_start(out=x_tile[:], in_=x_view[:, :, c * x_cols : (c + 1) * x_cols])
             x_tiles.append(x_tile)
+
+        for a in range(PASSES // PLANES):
             for quad in range(4):
                 nc.sync.dma_start(
-                    out=w_planes[32 * quad : 32 * quad + 4 * PLANES, c, :].bitcast(I32),
-                    in_=W_scales[PLANES * c : PLANES * (c + 1), 4 * quad : 4 * quad + 4, :].bitcast(I32),
+                    out=w_planes[32 * quad : 32 * quad + 4 * PLANES, a, :].bitcast(I32),
+                    in_=W_scales[PLANES * a : PLANES * (a + 1), 4 * quad : 4 * quad + 4, :].bitcast(I32),
                 )
 
         x_codes = keep.tile([P, PASSES * TOKENS], U32, align_bytes=64)

@@ -32,11 +32,12 @@ X_CHUNK = 4
 X_CHUNKS = PASSES // X_CHUNK
 PAIR = 2
 PLANES = 4
+assert X_CHUNK == PLANES
 W_CHUNK = 2
 W_BUFS = 8
 LATE_PASSES = 12
 GROUP_TILES = 2
-SMALLEST_VARIANCE_SUM = 1e-30
+SMALLEST_SQUARE_SUM = 1e-28
 
 FLOPS = 2 * TOKENS * FEATURES * OUTPUTS
 
@@ -58,7 +59,7 @@ def tile_linearnnencoder_k_kernel(tc, x, W_words, W_scales, b, out):
         nc.vector.memset(w_planes[:].bitcast(I32), 0)
 
         warm = keep.tile([P, 1], F32)
-        nc.vector.memset(warm[:], 0.0)
+        nc.vector.memset(warm[:], 1.0)
         nc.scalar.activation(out=warm[:], in_=warm[:], func=ACT.Gelu)
 
         b_rows = keep.tile([OUT_TILES, P], BF16)
@@ -78,12 +79,10 @@ def tile_linearnnencoder_k_kernel(tc, x, W_words, W_scales, b, out):
             x_tile = keep.tile([P, TOKEN_TILES, x_cols], BF16, name="x%d" % c)
             nc.sync.dma_start(out=x_tile[:], in_=x_view[:, :, c * x_cols : (c + 1) * x_cols])
             x_tiles.append(x_tile)
-
-        for a in range(PASSES // PLANES):
             for quad in range(4):
                 nc.sync.dma_start(
-                    out=w_planes[32 * quad : 32 * quad + 4 * PLANES, a, :].bitcast(I32),
-                    in_=W_scales[PLANES * a : PLANES * (a + 1), 4 * quad : 4 * quad + 4, :].bitcast(I32),
+                    out=w_planes[32 * quad : 32 * quad + 4 * PLANES, c, :].bitcast(I32),
+                    in_=W_scales[PLANES * c : PLANES * (c + 1), 4 * quad : 4 * quad + 4, :].bitcast(I32),
                 )
 
         x_codes = keep.tile([P, PASSES * TOKENS], U32, align_bytes=64)
@@ -172,11 +171,13 @@ def tile_linearnnencoder_k_kernel(tc, x, W_words, W_scales, b, out):
                         stop=(g == PASSES - 1),
                     )
 
-        results = keep.tile([P, SAMPLES, 2, OUT_TILES], F32)
-        variance = keep.tile([P, SAMPLES, OUT_TILES], F32)
+        neg_totals = keep.tile([P, SAMPLES, OUT_TILES], F32)
+        square_sums = keep.tile([P, SAMPLES, OUT_TILES], F32)
         mask = keep.tile([P, TOKENS], F32)
-        inv_n = keep.tile([P, SAMPLES], F32)
-        inv_n1 = keep.tile([P, SAMPLES], F32)
+        count = keep.tile([P, SAMPLES], F32)
+
+        def by_sample(row):
+            return row[:].rearrange("p (s t) -> p s t", t=SAMPLE_TOKENS)
 
         def make_mask():
             mask_bank = psum.tile([P, TOKENS], F32, tag="bank0")
@@ -189,17 +190,7 @@ def tile_linearnnencoder_k_kernel(tc, x, W_words, W_scales, b, out):
                     stop=True,
                 )
             nc.vector.tensor_copy(out=mask[:], in_=mask_bank[:])
-            count = keep.tile([P, SAMPLES], F32)
             nc.vector.tensor_reduce(out=count[:], in_=by_sample(mask), axis=AXIS.X, op=ALU.add)
-            nc.vector.tensor_scalar_max(out=inv_n[:], in0=count[:], scalar1=1.0)
-            nc.vector.reciprocal(out=inv_n[:], in_=inv_n[:])
-            nc.vector.tensor_scalar(
-                out=inv_n1[:], in0=count[:], scalar1=-1.0, scalar2=1.0, op0=ALU.add, op1=ALU.max
-            )
-            nc.vector.reciprocal(out=inv_n1[:], in_=inv_n1[:])
-
-        def by_sample(row):
-            return row[:].rearrange("p (s t) -> p s t", t=SAMPLE_TOKENS)
 
         def gelu(group):
             ys = []
@@ -213,49 +204,68 @@ def tile_linearnnencoder_k_kernel(tc, x, W_words, W_scales, b, out):
             for j, y in ys:
                 nc.vector.tensor_tensor(out=y[:], in0=y[:], in1=mask[:], op=ALU.mult)
             for j, y in ys:
-                total = y_pool.tile([P, SAMPLES], F32)
-                nc.vector.tensor_reduce(out=total[:], in_=by_sample(y), axis=AXIS.X, op=ALU.add)
-                nc.vector.tensor_tensor(out=results[:, :, 1, j], in0=total[:], in1=inv_n[:], op=ALU.mult)
-            for j, y in ys:
-                nc.vector.tensor_tensor(
-                    out=by_sample(y),
-                    in0=by_sample(y),
-                    in1=results[:, :, 1, j].unsqueeze(2).to_broadcast([P, SAMPLES, SAMPLE_TOKENS]),
-                    op=ALU.subtract,
+                nc.vector.tensor_reduce(
+                    out=neg_totals[:, :, j], in_=by_sample(y), axis=AXIS.X, op=ALU.add, negate=True
                 )
+            for j, y in ys:
+                for s in range(SAMPLES):
+                    tokens = slice(s * SAMPLE_TOKENS, (s + 1) * SAMPLE_TOKENS)
+                    nc.scalar.activation(
+                        out=y[:, tokens],
+                        in_=y[:, tokens],
+                        func=ACT.Square,
+                        scale=count[:, s : s + 1],
+                        bias=neg_totals[:, s, j : j + 1],
+                    )
             for j, y in ys:
                 nc.vector.tensor_tensor(out=y[:], in0=y[:], in1=mask[:], op=ALU.mult)
-                nc.scalar.activation(out=y[:], in_=y[:], func=ACT.Square)
             for j, y in ys:
-                squares = y_pool.tile([P, SAMPLES], F32)
-                nc.vector.tensor_reduce(out=squares[:], in_=by_sample(y), axis=AXIS.X, op=ALU.add)
-                nc.vector.scalar_tensor_tensor(
-                    out=variance[:, :, j],
-                    in0=squares[:],
-                    scalar=SMALLEST_VARIANCE_SUM,
-                    in1=inv_n1[:],
-                    op0=ALU.max,
-                    op1=ALU.mult,
-                )
+                nc.vector.tensor_reduce(out=square_sums[:, :, j], in_=by_sample(y), axis=AXIS.X, op=ALU.add)
 
-        def root(first_tile, tiles):
-            cols = slice(first_tile, first_tile + tiles)
-            nc.scalar.activation(out=results[:, :, 0, cols], in_=variance[:, :, cols], func=ACT.Sqrt)
+        neg_inv_n = keep.tile([P, SAMPLES], F32)
+        inv_var = keep.tile([P, SAMPLES], F32)
+
+        def make_divisors():
+            nc.vector.tensor_scalar_max(out=neg_inv_n[:], in0=count[:], scalar1=1.0)
+            nc.vector.tensor_scalar(
+                out=inv_var[:], in0=count[:], scalar1=-1.0, scalar2=1.0, op0=ALU.add, op1=ALU.max
+            )
+            nc.vector.tensor_tensor(out=inv_var[:], in0=inv_var[:], in1=neg_inv_n[:], op=ALU.mult)
+            nc.vector.tensor_tensor(out=inv_var[:], in0=inv_var[:], in1=neg_inv_n[:], op=ALU.mult)
+            nc.vector.reciprocal(out=inv_var[:], in_=inv_var[:])
+            nc.vector.reciprocal(out=neg_inv_n[:], in_=neg_inv_n[:])
+            nc.vector.tensor_scalar_mul(out=neg_inv_n[:], in0=neg_inv_n[:], scalar1=-1.0)
 
         early = PASSES - LATE_PASSES
         for first_pass in range(0, early, W_CHUNK):
             multiply(first_pass, 0, OUT_TILES)
-        last_group = OUT_TILES - GROUP_TILES
         for first_tile in range(0, OUT_TILES, GROUP_TILES):
             for first_pass in range(early, PASSES, W_CHUNK):
                 multiply(first_pass, first_tile, GROUP_TILES)
             ys = gelu(range(first_tile, first_tile + GROUP_TILES))
             if first_tile == 0:
                 make_mask()
-            if first_tile == last_group:
-                root(0, last_group)
             statistics(ys)
-        root(last_group, GROUP_TILES)
+            if first_tile == 0:
+                make_divisors()
+
+        nc.scalar.activation(out=warm[:], in_=warm[:], func=ACT.Sqrt)
+
+        def over_tiles(row):
+            return row[:].unsqueeze(2).to_broadcast([P, SAMPLES, OUT_TILES])
+
+        results = keep.tile([P, SAMPLES, 2, OUT_TILES], F32)
+        variance = keep.tile([P, SAMPLES, OUT_TILES], F32)
+        nc.vector.scalar_tensor_tensor(
+            out=variance[:],
+            in0=square_sums[:],
+            scalar=SMALLEST_SQUARE_SUM,
+            in1=over_tiles(inv_var),
+            op0=ALU.max,
+            op1=ALU.mult,
+        )
+        nc.scalar.activation(out=results[:, :, 0, :], in_=variance[:], func=ACT.Sqrt)
+        nc.vector.tensor_tensor(out=results[:, :, 1, :], in0=neg_totals[:], in1=over_tiles(neg_inv_n), op=ALU.mult)
 
         out_bank = psum.tile([P, P], F32, tag="bank1")
         nc.tensor.transpose(out_bank[:], results[:].rearrange("p s i j -> p (s i j)"), ident[:])

@@ -35,7 +35,9 @@ PLANES = 4
 assert X_CHUNK == PLANES
 W_CHUNK = 2
 W_BUFS = 8
-LATE_PASSES = 12
+LATE_PASSES = 8
+LATE_CHUNK = 4
+LATE_BUFS = 4
 GROUP_TILES = 2
 SMALLEST_SQUARE_SUM = 1e-28
 
@@ -148,19 +150,20 @@ def tile_linearnnencoder_k_kernel(tc, x, W_words, W_scales, b, out):
 
         acc = [psum.tile([P, TOKENS], F32, tag="bank%d" % j, name="acc%d" % j) for j in range(OUT_TILES)]
 
-        def multiply(first_pass, first_tile, tiles):
-            w_tile = w_pool.tile([P, W_CHUNK, tiles * P], U32, tag="w%d" % tiles, align_bytes=64)
+        def multiply(w_tile, first_pass, first_tile):
+            passes = w_tile.shape[1]
+            tiles = w_tile.shape[2] // P
             columns = slice(first_tile * P, (first_tile + tiles) * P)
             nc.sync.dma_start(
                 out=w_tile[:].bitcast(I32),
-                in_=W_words[first_pass : first_pass + W_CHUNK, :, columns, :]
+                in_=W_words[first_pass : first_pass + passes, :, columns, :]
                 .rearrange("g p n t -> p g (n t)")
                 .bitcast(I32),
             )
-            for i in range(W_CHUNK):
-                g = first_pass + i
-                for jj in range(tiles):
-                    j = first_tile + jj
+            for jj in range(tiles):
+                j = first_tile + jj
+                for i in range(passes):
+                    g = first_pass + i
                     nc.tensor.matmul_mx(
                         out=acc[j][:],
                         lhsT=w_tile[:, i, jj * P : (jj + 1) * P].bitcast(FP8X4),
@@ -238,10 +241,12 @@ def tile_linearnnencoder_k_kernel(tc, x, W_words, W_scales, b, out):
 
         early = PASSES - LATE_PASSES
         for first_pass in range(0, early, W_CHUNK):
-            multiply(first_pass, 0, OUT_TILES)
+            w_rows = w_pool.tile([P, W_CHUNK, OUTPUTS], U32, align_bytes=64)
+            multiply(w_rows, first_pass, 0)
         for first_tile in range(0, OUT_TILES, GROUP_TILES):
-            for first_pass in range(early, PASSES, W_CHUNK):
-                multiply(first_pass, first_tile, GROUP_TILES)
+            for first_pass in range(early, PASSES, LATE_CHUNK):
+                w_group = w_pool.tile([P, LATE_CHUNK, GROUP_TILES * P], U32, bufs=LATE_BUFS, align_bytes=64)
+                multiply(w_group, first_pass, first_tile)
             ys = gelu(range(first_tile, first_tile + GROUP_TILES))
             if first_tile == 0:
                 make_mask()

@@ -17,7 +17,6 @@ P = 128
 PACK = 4
 K_PASS = P * PACK
 WORDS_PASS = K_PASS // 2
-BANKS = 8
 
 SAMPLES = 8
 SAMPLE_TOKENS = 32
@@ -30,14 +29,15 @@ OUT_TILES = OUTPUTS // P
 
 X_CHUNK = 4
 X_CHUNKS = PASSES // X_CHUNK
-PAIR = 2
+RUN = 2
+RUNS = PASSES // RUN
+MX_LAG = 2
 PLANES = 4
 assert X_CHUNK == PLANES
+HALF_TILES = OUT_TILES // 2
 W_CHUNK = 2
 W_BUFS = 8
-LATE_PASSES = 8
-LATE_CHUNK = 4
-LATE_BUFS = 4
+LATE_PASSES = 12
 GROUP_TILES = 2
 SMALLEST_SQUARE_SUM = 1e-28
 
@@ -51,7 +51,7 @@ def tile_linearnnencoder_k_kernel(tc, x, W_words, W_scales, b, out):
         keep = stack.enter_context(tc.tile_pool(name="keep", bufs=1))
         stage = stack.enter_context(tc.tile_pool(name="stage", bufs=4))
         w_pool = stack.enter_context(tc.tile_pool(name="w_pool", bufs=W_BUFS))
-        y_pool = stack.enter_context(tc.tile_pool(name="y_pool", bufs=4))
+        y_pool = stack.enter_context(tc.tile_pool(name="y_pool", bufs=HALF_TILES + GROUP_TILES))
         psum = stack.enter_context(tc.psum_pool(name="psum", bufs=1))
 
         ident = keep.tile([P, P], F32)
@@ -74,9 +74,40 @@ def tile_linearnnencoder_k_kernel(tc, x, W_words, W_scales, b, out):
         b_col = keep.tile([P, OUT_TILES], F32)
         nc.vector.tensor_copy(out=b_col[:], in_=b_bank[:, 0:OUT_TILES])
 
+        acc = {}
+
+        def open_groups(tiles):
+            for j in tiles:
+                acc[j] = psum.tile([P, TOKENS], F32, tag="bank%d" % j, name="acc%d" % j)
+
+        def load_w(first_pass, passes, first_tile, tiles):
+            w_tile = w_pool.tile([P, passes, tiles * P], U32, align_bytes=64)
+            nc.sync.dma_start(
+                out=w_tile[:].bitcast(I32),
+                in_=W_words[first_pass : first_pass + passes, :, first_tile * P : (first_tile + tiles) * P, :]
+                .rearrange("g p n t -> p g (n t)")
+                .bitcast(I32),
+            )
+            return w_tile
+
+        def multiply(w_tile, first_pass, passes, first_tile):
+            for g in passes:
+                for jj in range(w_tile.shape[2] // P):
+                    j = first_tile + jj
+                    nc.tensor.matmul_mx(
+                        out=acc[j][:],
+                        lhsT=w_tile[:, g - first_pass, jj * P : (jj + 1) * P].bitcast(FP8X4),
+                        lhsT_scale=w_planes[4 * (g % PLANES) : P, g // PLANES, j * P : (j + 1) * P],
+                        rhs=x_codes[:, g * TOKENS : (g + 1) * TOKENS].bitcast(FP8X4),
+                        rhs_scale=x_scales[:, g * TOKENS : (g + 1) * TOKENS],
+                        start=(g == 0),
+                        stop=(g == PASSES - 1),
+                    )
+
         x_view = x.flatten_outer_dims().rearrange("(h p) k -> p h k", p=P)
         x_cols = X_CHUNK * K_PASS
         x_tiles = []
+        left_tiles = []
         for c in range(X_CHUNKS):
             x_tile = keep.tile([P, TOKEN_TILES, x_cols], BF16, name="x%d" % c)
             nc.sync.dma_start(out=x_tile[:], in_=x_view[:, :, c * x_cols : (c + 1) * x_cols])
@@ -86,13 +117,14 @@ def tile_linearnnencoder_k_kernel(tc, x, W_words, W_scales, b, out):
                     out=w_planes[32 * quad : 32 * quad + 4 * PLANES, c, :].bitcast(I32),
                     in_=W_scales[PLANES * c : PLANES * (c + 1), 4 * quad : 4 * quad + 4, :].bitcast(I32),
                 )
+            left_tiles.append(load_w(c * X_CHUNK, X_CHUNK, 0, HALF_TILES))
 
         x_codes = keep.tile([P, PASSES * TOKENS], U32, align_bytes=64)
         x_scales = keep.tile([P, PASSES * TOKENS], U8, align_bytes=64)
 
         def transpose_pass(g, grouped_pass):
             first_word = (g % X_CHUNK) * WORDS_PASS
-            bank = psum.tile([P, 2, TOKENS], F32, tag="bank%d" % (g % BANKS), name="x_bank")
+            bank = psum.tile([P, 2, TOKENS], F32, tag="bank%d" % (HALF_TILES + g % HALF_TILES), name="x_bank")
             for h in range(TOKEN_TILES):
                 words = x_tiles[g // X_CHUNK][:, h, :].bitcast(F32)
                 for u in range(2):
@@ -104,75 +136,59 @@ def tile_linearnnencoder_k_kernel(tc, x, W_words, W_scales, b, out):
             copy = nc.vector.tensor_copy if g % 4 == 3 else nc.scalar.copy
             copy(out=grouped_pass.bitcast(F32), in_=bank[:].rearrange("p u r -> p r u"))
 
-        def quantise_pair(q, grouped):
-            cols = slice(q * PAIR * TOKENS, (q + 1) * PAIR * TOKENS)
+        def quantise_run(r, grouped):
+            cols = slice(r * RUN * TOKENS, (r + 1) * RUN * TOKENS)
             nc.vector.quantize_mx(
                 out=x_codes[:, cols].bitcast(FP8X4),
                 scales=x_scales[:, cols],
                 in_=grouped[:].rearrange("p g r t -> p (g r t)"),
             )
 
-        copied = None
-        for q in range(PASSES // PAIR):
-            grouped = stage.tile([P, PAIR, TOKENS, PACK], BF16, align_bytes=64)
-            for i in range(PAIR):
-                transpose_pass(PAIR * q + i, grouped[:, i])
-            if copied is not None:
-                quantise_pair(q - 1, copied)
-            copied = grouped
-        quantise_pair(PASSES // PAIR - 1, copied)
+        differs = keep.tile([P, RUNS], F32)
+        distance = keep.tile([P, RUNS], F32)
 
-        differs = keep.tile([P, X_CHUNKS], F32)
-        distance = keep.tile([P, X_CHUNKS], F32)
-        for c in range(X_CHUNKS):
+        def padding_test(r):
+            x_tile = x_tiles[r * RUN // X_CHUNK]
+            first = (r * RUN % X_CHUNK) * K_PASS
+            cols = slice(first, first + RUN * K_PASS)
             nc.vector.tensor_scalar(
-                out=x_tiles[c][:, 0, :],
-                in0=x_tiles[c][:, 0, :],
+                out=x_tile[:, 0, cols],
+                in0=x_tile[:, 0, cols],
                 scalar1=-1.0,
                 scalar2=None,
                 op0=ALU.not_equal,
                 op1=ALU.max,
-                accum_out=differs[:, c : c + 1],
+                accum_out=differs[:, r : r + 1],
             )
             nc.scalar.activation(
-                out=x_tiles[c][:, 1, :],
-                in_=x_tiles[c][:, 1, :],
+                out=x_tile[:, 1, cols],
+                in_=x_tile[:, 1, cols],
                 func=ACT.Square,
                 bias=1.0,
                 scale=1.0,
-                accum_out=distance[:, c : c + 1],
+                accum_out=distance[:, r : r + 1],
             )
+
+        open_groups(range(HALF_TILES))
+        grouped_tiles = {}
+        for r in range(RUNS + MX_LAG):
+            if r < RUNS:
+                grouped_tiles[r] = stage.tile([P, RUN, TOKENS, PACK], BF16, name="grouped", align_bytes=64)
+                for i in range(RUN):
+                    transpose_pass(RUN * r + i, grouped_tiles[r][:, i])
+            if 1 <= r <= RUNS:
+                quantise_run(r - 1, grouped_tiles[r - 1])
+                padding_test(r - 1)
+            if r >= MX_LAG:
+                first_pass = (r - MX_LAG) * RUN
+                c = first_pass // X_CHUNK
+                multiply(left_tiles[c], c * X_CHUNK, range(first_pass, first_pass + RUN), 0)
+
         valid = keep.tile([P, TOKEN_TILES], F32)
         row_distance = keep.tile([P, 1], F32)
         nc.vector.tensor_reduce(out=valid[:, 0:1], in_=differs[:], axis=AXIS.X, op=ALU.max)
         nc.vector.tensor_reduce(out=row_distance[:], in_=distance[:], axis=AXIS.X, op=ALU.add)
         nc.vector.tensor_single_scalar(out=valid[:, 1:2], in_=row_distance[:], scalar=0.0, op=ALU.not_equal)
-
-        acc = [psum.tile([P, TOKENS], F32, tag="bank%d" % j, name="acc%d" % j) for j in range(OUT_TILES)]
-
-        def multiply(w_tile, first_pass, first_tile):
-            passes = w_tile.shape[1]
-            tiles = w_tile.shape[2] // P
-            columns = slice(first_tile * P, (first_tile + tiles) * P)
-            nc.sync.dma_start(
-                out=w_tile[:].bitcast(I32),
-                in_=W_words[first_pass : first_pass + passes, :, columns, :]
-                .rearrange("g p n t -> p g (n t)")
-                .bitcast(I32),
-            )
-            for jj in range(tiles):
-                j = first_tile + jj
-                for i in range(passes):
-                    g = first_pass + i
-                    nc.tensor.matmul_mx(
-                        out=acc[j][:],
-                        lhsT=w_tile[:, i, jj * P : (jj + 1) * P].bitcast(FP8X4),
-                        lhsT_scale=w_planes[4 * (g % PLANES) : P, g // PLANES, j * P : (j + 1) * P],
-                        rhs=x_codes[:, g * TOKENS : (g + 1) * TOKENS].bitcast(FP8X4),
-                        rhs_scale=x_scales[:, g * TOKENS : (g + 1) * TOKENS],
-                        start=(g == 0),
-                        stop=(g == PASSES - 1),
-                    )
 
         neg_totals = keep.tile([P, SAMPLES, OUT_TILES], F32)
         square_sums = keep.tile([P, SAMPLES, OUT_TILES], F32)
@@ -239,20 +255,21 @@ def tile_linearnnencoder_k_kernel(tc, x, W_words, W_scales, b, out):
             nc.vector.reciprocal(out=neg_inv_n[:], in_=neg_inv_n[:])
             nc.vector.tensor_scalar_mul(out=neg_inv_n[:], in0=neg_inv_n[:], scalar1=-1.0)
 
+        left_ys = gelu(range(HALF_TILES))
+        open_groups(range(HALF_TILES, OUT_TILES))
         early = PASSES - LATE_PASSES
-        for first_pass in range(0, early, W_CHUNK):
-            w_rows = w_pool.tile([P, W_CHUNK, OUTPUTS], U32, align_bytes=64)
-            multiply(w_rows, first_pass, 0)
-        for first_tile in range(0, OUT_TILES, GROUP_TILES):
-            for first_pass in range(early, PASSES, LATE_CHUNK):
-                w_group = w_pool.tile([P, LATE_CHUNK, GROUP_TILES * P], U32, bufs=LATE_BUFS, align_bytes=64)
-                multiply(w_group, first_pass, first_tile)
-            ys = gelu(range(first_tile, first_tile + GROUP_TILES))
-            if first_tile == 0:
+        for first_pass in range(0, early, X_CHUNK):
+            w_tile = load_w(first_pass, X_CHUNK, HALF_TILES, HALF_TILES)
+            multiply(w_tile, first_pass, range(first_pass, first_pass + X_CHUNK), HALF_TILES)
+            if first_pass == 0:
                 make_mask()
-            statistics(ys)
-            if first_tile == 0:
+                statistics(left_ys)
                 make_divisors()
+        for first_tile in range(HALF_TILES, OUT_TILES, GROUP_TILES):
+            for first_pass in range(early, PASSES, W_CHUNK):
+                w_tile = load_w(first_pass, W_CHUNK, first_tile, GROUP_TILES)
+                multiply(w_tile, first_pass, range(first_pass, first_pass + W_CHUNK), first_tile)
+            statistics(gelu(range(first_tile, first_tile + GROUP_TILES)))
 
         nc.scalar.activation(out=warm[:], in_=warm[:], func=ACT.Sqrt)
 

@@ -35,10 +35,14 @@ MX_LAG = 2
 PLANES = 4
 assert X_CHUNK == PLANES
 HALF_TILES = OUT_TILES // 2
-W_CHUNK = 2
-W_BUFS = 8
-LATE_PASSES = 12
+EARLY = 12
+FULL_CHUNK = 2
+MASK_AFTER = 2
+LEFT_STRIDE = 2
+LATE_CHUNK = 4
 GROUP_TILES = 2
+RING = 18
+PAD_WORD = -1.0058441162109375
 SMALLEST_SQUARE_SUM = 1e-28
 
 FLOPS = 2 * TOKENS * FEATURES * OUTPUTS
@@ -50,7 +54,7 @@ def tile_linearnnencoder_k_kernel(tc, x, W_words, W_scales, b, out):
         stack.enter_context(tc.manual_schedule())
         keep = stack.enter_context(tc.tile_pool(name="keep", bufs=1))
         stage = stack.enter_context(tc.tile_pool(name="stage", bufs=4))
-        w_pool = stack.enter_context(tc.tile_pool(name="w_pool", bufs=W_BUFS))
+        ring = stack.enter_context(tc.tile_pool(name="ring", bufs=RING))
         y_pool = stack.enter_context(tc.tile_pool(name="y_pool", bufs=HALF_TILES + GROUP_TILES))
         psum = stack.enter_context(tc.psum_pool(name="psum", bufs=1))
 
@@ -81,43 +85,67 @@ def tile_linearnnencoder_k_kernel(tc, x, W_words, W_scales, b, out):
                 acc[j] = psum.tile([P, TOKENS], F32, tag="bank%d" % j, name="acc%d" % j)
 
         def load_w(first_pass, passes, first_tile, tiles):
-            w_tile = w_pool.tile([P, passes, tiles * P], U32, align_bytes=64)
+            loaded = ring.tile([P, passes, tiles * P], U32, align_bytes=64, tag="load", name="w_load")
             nc.sync.dma_start(
-                out=w_tile[:].bitcast(I32),
+                out=loaded[:].bitcast(I32),
                 in_=W_words[first_pass : first_pass + passes, :, first_tile * P : (first_tile + tiles) * P, :]
                 .rearrange("g p n t -> p g (n t)")
                 .bitcast(I32),
             )
-            return w_tile
+            return loaded, first_pass, first_tile
 
-        def multiply(w_tile, first_pass, passes, first_tile):
-            for g in passes:
-                for jj in range(w_tile.shape[2] // P):
-                    j = first_tile + jj
-                    nc.tensor.matmul_mx(
-                        out=acc[j][:],
-                        lhsT=w_tile[:, g - first_pass, jj * P : (jj + 1) * P].bitcast(FP8X4),
-                        lhsT_scale=w_planes[4 * (g % PLANES) : P, g // PLANES, j * P : (j + 1) * P],
-                        rhs=x_codes[:, g * TOKENS : (g + 1) * TOKENS].bitcast(FP8X4),
-                        rhs_scale=x_scales[:, g * TOKENS : (g + 1) * TOKENS],
-                        start=(g == 0),
-                        stop=(g == PASSES - 1),
-                    )
-
-        x_view = x.flatten_outer_dims().rearrange("(h p) k -> p h k", p=P)
-        x_cols = X_CHUNK * K_PASS
-        x_tiles = []
-        left_tiles = []
-        for c in range(X_CHUNKS):
-            x_tile = keep.tile([P, TOKEN_TILES, x_cols], BF16, name="x%d" % c)
-            nc.sync.dma_start(out=x_tile[:], in_=x_view[:, :, c * x_cols : (c + 1) * x_cols])
-            x_tiles.append(x_tile)
+        def load_scales(c):
             for quad in range(4):
                 nc.sync.dma_start(
                     out=w_planes[32 * quad : 32 * quad + 4 * PLANES, c, :].bitcast(I32),
                     in_=W_scales[PLANES * c : PLANES * (c + 1), 4 * quad : 4 * quad + 4, :].bitcast(I32),
                 )
-            left_tiles.append(load_w(c * X_CHUNK, X_CHUNK, 0, HALF_TILES))
+
+        def multiply(load, passes, tiles):
+            loaded, first_pass, first_tile = load
+            for g in passes:
+                for j in tiles:
+                    cols = slice((j - first_tile) * P, (j - first_tile + 1) * P)
+                    nc.tensor.matmul_mx(
+                        out=acc[j][:],
+                        lhsT=loaded[:, g - first_pass, cols].bitcast(FP8X4),
+                        lhsT_scale=w_planes[4 * (g % PLANES) : P, g // PLANES, j * P : (j + 1) * P],
+                        rhs=x_codes[:, g * TOKENS : (g + 1) * TOKENS].bitcast(FP8X4),
+                        rhs_scale=x_scales[:, g * TOKENS : (g + 1) * TOKENS],
+                        start=(g == (0 if j < HALF_TILES else EARLY)),
+                        stop=(g == (PASSES if j < HALF_TILES else EARLY) - 1),
+                    )
+
+        left = range(HALF_TILES)
+        right = range(HALF_TILES, OUT_TILES)
+
+        x_view = x.flatten_outer_dims().rearrange("(h p) k -> p h k", p=P)
+        x_cols = X_CHUNK * K_PASS
+        x_tiles = []
+        left_loads = []
+
+        def load_x(c):
+            x_tile = ring.tile([P, TOKEN_TILES, x_cols], BF16, align_bytes=64, tag="load", name="x_load")
+            nc.sync.dma_start(out=x_tile[:], in_=x_view[:, :, c * x_cols : (c + 1) * x_cols])
+            x_tiles.append(x_tile)
+
+        def load_left(c):
+            load_scales(c)
+            left_loads.append(load_w(c * PLANES, PLANES, 0, HALF_TILES))
+
+        def load_full(first_pass):
+            if first_pass % PLANES == 0:
+                load_scales(first_pass // PLANES)
+            return load_w(first_pass, FULL_CHUNK, 0, OUT_TILES)
+
+        for c in range(X_CHUNKS):
+            load_x(c)
+            if c % LEFT_STRIDE == 0 and c // LEFT_STRIDE < EARLY // PLANES:
+                load_left(c // LEFT_STRIDE)
+        full_loads = [
+            load_full(first_pass)
+            for first_pass in range(EARLY, EARLY + FULL_CHUNK * (RING - X_CHUNKS - EARLY // PLANES), FULL_CHUNK)
+        ]
 
         x_codes = keep.tile([P, PASSES * TOKENS], U32, align_bytes=64)
         x_scales = keep.tile([P, PASSES * TOKENS], U8, align_bytes=64)
@@ -146,43 +174,46 @@ def tile_linearnnencoder_k_kernel(tc, x, W_words, W_scales, b, out):
 
         differs = keep.tile([P, RUNS], F32)
         distance = keep.tile([P, RUNS], F32)
+        minus_pad = keep.tile([P, 1], F32)
+        nc.vector.memset(minus_pad[:], -PAD_WORD)
 
         def padding_test(r):
             x_tile = x_tiles[r * RUN // X_CHUNK]
-            first = (r * RUN % X_CHUNK) * K_PASS
-            cols = slice(first, first + RUN * K_PASS)
+            first = (r * RUN % X_CHUNK) * WORDS_PASS
+            cols = slice(first, first + RUN * WORDS_PASS)
+            vector_words = x_tile[:, 0, :].bitcast(F32)[:, cols]
+            scalar_words = x_tile[:, 1, :].bitcast(F32)[:, cols]
             nc.vector.tensor_scalar(
-                out=x_tile[:, 0, cols],
-                in0=x_tile[:, 0, cols],
-                scalar1=-1.0,
+                out=vector_words,
+                in0=vector_words,
+                scalar1=PAD_WORD,
                 scalar2=None,
                 op0=ALU.not_equal,
                 op1=ALU.max,
                 accum_out=differs[:, r : r + 1],
             )
             nc.scalar.activation(
-                out=x_tile[:, 1, cols],
-                in_=x_tile[:, 1, cols],
+                out=scalar_words,
+                in_=scalar_words,
                 func=ACT.Square,
-                bias=1.0,
+                bias=minus_pad[:],
                 scale=1.0,
                 accum_out=distance[:, r : r + 1],
             )
 
-        open_groups(range(HALF_TILES))
+        open_groups(left)
         grouped_tiles = {}
-        for r in range(RUNS + MX_LAG):
+        for r in range(RUNS + 1):
             if r < RUNS:
                 grouped_tiles[r] = stage.tile([P, RUN, TOKENS, PACK], BF16, name="grouped", align_bytes=64)
                 for i in range(RUN):
                     transpose_pass(RUN * r + i, grouped_tiles[r][:, i])
-            if 1 <= r <= RUNS:
+            if r >= 1:
                 quantise_run(r - 1, grouped_tiles[r - 1])
                 padding_test(r - 1)
-            if r >= MX_LAG:
-                first_pass = (r - MX_LAG) * RUN
-                c = first_pass // X_CHUNK
-                multiply(left_tiles[c], c * X_CHUNK, range(first_pass, first_pass + RUN), 0)
+            g = r - MX_LAG
+            if 0 <= g < EARLY:
+                multiply(left_loads[g // PLANES], [g], left)
 
         valid = keep.tile([P, TOKEN_TILES], F32)
         row_distance = keep.tile([P, 1], F32)
@@ -199,7 +230,7 @@ def tile_linearnnencoder_k_kernel(tc, x, W_words, W_scales, b, out):
             return row[:].rearrange("p (s t) -> p s t", t=SAMPLE_TOKENS)
 
         def make_mask():
-            mask_bank = psum.tile([P, TOKENS], F32, tag="bank0")
+            mask_bank = psum.tile([P, TOKENS], F32, tag="bank%d" % HALF_TILES)
             for h in range(TOKEN_TILES):
                 nc.tensor.matmul(
                     out=mask_bank[:, h * P : (h + 1) * P],
@@ -255,21 +286,28 @@ def tile_linearnnencoder_k_kernel(tc, x, W_words, W_scales, b, out):
             nc.vector.reciprocal(out=neg_inv_n[:], in_=neg_inv_n[:])
             nc.vector.tensor_scalar_mul(out=neg_inv_n[:], in0=neg_inv_n[:], scalar1=-1.0)
 
-        left_ys = gelu(range(HALF_TILES))
-        open_groups(range(HALF_TILES, OUT_TILES))
-        early = PASSES - LATE_PASSES
-        for first_pass in range(0, early, X_CHUNK):
-            w_tile = load_w(first_pass, X_CHUNK, HALF_TILES, HALF_TILES)
-            multiply(w_tile, first_pass, range(first_pass, first_pass + X_CHUNK), HALF_TILES)
-            if first_pass == 0:
-                make_mask()
-                statistics(left_ys)
-                make_divisors()
-        for first_tile in range(HALF_TILES, OUT_TILES, GROUP_TILES):
-            for first_pass in range(early, PASSES, W_CHUNK):
-                w_tile = load_w(first_pass, W_CHUNK, first_tile, GROUP_TILES)
-                multiply(w_tile, first_pass, range(first_pass, first_pass + W_CHUNK), first_tile)
-            statistics(gelu(range(first_tile, first_tile + GROUP_TILES)))
+        for load in full_loads[:MASK_AFTER]:
+            multiply(load, range(load[1], load[1] + FULL_CHUNK), left)
+        make_mask()
+        make_divisors()
+        open_groups(right)
+        for load in full_loads[:MASK_AFTER]:
+            multiply(load, range(load[1], load[1] + FULL_CHUNK), right)
+        for first_pass in range(EARLY + FULL_CHUNK * len(full_loads), PASSES, FULL_CHUNK):
+            full_loads.append(load_full(first_pass))
+        late_loads = [
+            (first_tile, [load_w(first_pass, LATE_CHUNK, first_tile, GROUP_TILES) for first_pass in range(0, EARLY, LATE_CHUNK)])
+            for first_tile in range(HALF_TILES, OUT_TILES, GROUP_TILES)
+        ]
+        for load in full_loads[MASK_AFTER:]:
+            multiply(load, range(load[1], load[1] + FULL_CHUNK), range(OUT_TILES))
+
+        statistics(gelu(left))
+        for first_tile, loads in late_loads:
+            group = range(first_tile, first_tile + GROUP_TILES)
+            for load in loads:
+                multiply(load, range(load[1], load[1] + LATE_CHUNK), group)
+            statistics(gelu(group))
 
         nc.scalar.activation(out=warm[:], in_=warm[:], func=ACT.Sqrt)
 

@@ -37,13 +37,13 @@ assert X_CHUNK == PLANES
 HALF_TILES = OUT_TILES // 2
 EARLY = 12
 FULL_CHUNK = 2
-MASK_AFTER = 2
+MASK_AFTER = 6
 LEFT_STRIDE = 2
 LATE_CHUNK = 4
 GROUP_TILES = 2
 RING = 18
 PAD_WORD = -1.0058441162109375
-SMALLEST_SQUARE_SUM = 1e-28
+TINY = 2.0**-100
 
 FLOPS = 2 * TOKENS * FEATURES * OUTPUTS
 
@@ -63,6 +63,9 @@ def tile_linearnnencoder_k_kernel(tc, x, W_words, W_scales, b, out):
 
         w_planes = keep.tile([P, PASSES // PLANES, OUTPUTS], U8, align_bytes=64)
         nc.vector.memset(w_planes[:].bitcast(I32), 0)
+
+        tiny = keep.tile([P, 1], F32)
+        nc.vector.memset(tiny[:], TINY)
 
         warm = keep.tile([P, 1], F32)
         nc.vector.memset(warm[:], 1.0)
@@ -117,7 +120,6 @@ def tile_linearnnencoder_k_kernel(tc, x, W_words, W_scales, b, out):
                     )
 
         left = range(HALF_TILES)
-        right = range(HALF_TILES, OUT_TILES)
 
         x_view = x.flatten_outer_dims().rearrange("(h p) k -> p h k", p=P)
         x_cols = X_CHUNK * K_PASS
@@ -150,19 +152,25 @@ def tile_linearnnencoder_k_kernel(tc, x, W_words, W_scales, b, out):
         x_codes = keep.tile([P, PASSES * TOKENS], U32, align_bytes=64)
         x_scales = keep.tile([P, PASSES * TOKENS], U8, align_bytes=64)
 
-        def transpose_pass(g, grouped_pass):
-            first_word = (g % X_CHUNK) * WORDS_PASS
-            bank = psum.tile([P, 2, TOKENS], F32, tag="bank%d" % (HALF_TILES + g % HALF_TILES), name="x_bank")
-            for h in range(TOKEN_TILES):
-                words = x_tiles[g // X_CHUNK][:, h, :].bitcast(F32)
-                for u in range(2):
-                    nc.tensor.transpose(
-                        bank[:, u, h * P : (h + 1) * P],
-                        words[:, first_word + u : first_word + WORDS_PASS : 2],
-                        ident[:],
-                    )
-            copy = nc.vector.tensor_copy if g % 4 == 3 else nc.scalar.copy
-            copy(out=grouped_pass.bitcast(F32), in_=bank[:].rearrange("p u r -> p r u"))
+        def sort_run(r):
+            sorted_words = stage.tile([P, TOKEN_TILES, 2, RUN * P], F32, name="sorted_words", align_bytes=64)
+            first_word = (r * RUN % X_CHUNK) * WORDS_PASS
+            words = x_tiles[r * RUN // X_CHUNK][:].rearrange("p h k -> p (h k)").bitcast(F32)
+            words = words.rearrange("p (h k) -> p h k", h=TOKEN_TILES)[:, :, first_word : first_word + RUN * WORDS_PASS]
+            nc.vector.tensor_copy(out=sorted_words[:], in_=words.rearrange("p h (w u) -> p h u w", u=2))
+            return sorted_words
+
+        def transpose_run(r, sorted_words, grouped):
+            for i in range(RUN):
+                bank = psum.tile([P, 2, TOKENS], F32, tag="bank%d" % (HALF_TILES + (RUN * r + i) % HALF_TILES), name="x_bank")
+                for h in range(TOKEN_TILES):
+                    for u in range(2):
+                        nc.tensor.transpose(
+                            bank[:, u, h * P : (h + 1) * P],
+                            sorted_words[:, h, u, i * P : (i + 1) * P],
+                            ident[:],
+                        )
+                nc.scalar.copy(out=grouped[:, i].bitcast(F32), in_=bank[:].rearrange("p u r -> p r u"))
 
         def quantise_run(r, grouped):
             cols = slice(r * RUN * TOKENS, (r + 1) * RUN * TOKENS)
@@ -172,17 +180,28 @@ def tile_linearnnencoder_k_kernel(tc, x, W_words, W_scales, b, out):
                 in_=grouped[:].rearrange("p g r t -> p (g r t)"),
             )
 
-        differs = keep.tile([P, RUNS], F32)
-        distance = keep.tile([P, RUNS], F32)
+        open_groups(left)
+        sorted_tiles = {0: sort_run(0)}
+        grouped_tiles = {}
+        for r in range(RUNS + 1):
+            if r < RUNS:
+                grouped_tiles[r] = stage.tile([P, RUN, TOKENS, PACK], BF16, name="grouped", align_bytes=64)
+                transpose_run(r, sorted_tiles[r], grouped_tiles[r])
+            if r >= 1:
+                quantise_run(r - 1, grouped_tiles[r - 1])
+            if r + 1 < RUNS:
+                sorted_tiles[r + 1] = sort_run(r + 1)
+            g = r - MX_LAG
+            if 0 <= g < EARLY:
+                multiply(left_loads[g // PLANES], [g], left)
+
+        differs = keep.tile([P, X_CHUNKS], F32)
+        distance = keep.tile([P, X_CHUNKS], F32)
         minus_pad = keep.tile([P, 1], F32)
         nc.vector.memset(minus_pad[:], -PAD_WORD)
-
-        def padding_test(r):
-            x_tile = x_tiles[r * RUN // X_CHUNK]
-            first = (r * RUN % X_CHUNK) * WORDS_PASS
-            cols = slice(first, first + RUN * WORDS_PASS)
-            vector_words = x_tile[:, 0, :].bitcast(F32)[:, cols]
-            scalar_words = x_tile[:, 1, :].bitcast(F32)[:, cols]
+        for c in range(X_CHUNKS):
+            vector_words = x_tiles[c][:, 0, :].bitcast(F32)
+            scalar_words = x_tiles[c][:, 1, :].bitcast(F32)
             nc.vector.tensor_scalar(
                 out=vector_words,
                 in0=vector_words,
@@ -190,7 +209,7 @@ def tile_linearnnencoder_k_kernel(tc, x, W_words, W_scales, b, out):
                 scalar2=None,
                 op0=ALU.not_equal,
                 op1=ALU.max,
-                accum_out=differs[:, r : r + 1],
+                accum_out=differs[:, c : c + 1],
             )
             nc.scalar.activation(
                 out=scalar_words,
@@ -198,22 +217,8 @@ def tile_linearnnencoder_k_kernel(tc, x, W_words, W_scales, b, out):
                 func=ACT.Square,
                 bias=minus_pad[:],
                 scale=1.0,
-                accum_out=distance[:, r : r + 1],
+                accum_out=distance[:, c : c + 1],
             )
-
-        open_groups(left)
-        grouped_tiles = {}
-        for r in range(RUNS + 1):
-            if r < RUNS:
-                grouped_tiles[r] = stage.tile([P, RUN, TOKENS, PACK], BF16, name="grouped", align_bytes=64)
-                for i in range(RUN):
-                    transpose_pass(RUN * r + i, grouped_tiles[r][:, i])
-            if r >= 1:
-                quantise_run(r - 1, grouped_tiles[r - 1])
-                padding_test(r - 1)
-            g = r - MX_LAG
-            if 0 <= g < EARLY:
-                multiply(left_loads[g // PLANES], [g], left)
 
         valid = keep.tile([P, TOKEN_TILES], F32)
         row_distance = keep.tile([P, 1], F32)
@@ -222,15 +227,20 @@ def tile_linearnnencoder_k_kernel(tc, x, W_words, W_scales, b, out):
         nc.vector.tensor_single_scalar(out=valid[:, 1:2], in_=row_distance[:], scalar=0.0, op=ALU.not_equal)
 
         neg_totals = keep.tile([P, SAMPLES, OUT_TILES], F32)
-        square_sums = keep.tile([P, SAMPLES, OUT_TILES], F32)
+        variances = keep.tile([P, 2, SAMPLES, OUT_TILES], F32)
+        nc.vector.memset(variances[:], 0.0)
+        means = keep.tile([P, 2, SAMPLES, OUT_TILES], F32)
+        final = keep.tile([P, P], F32)
+        half = SAMPLES * OUT_TILES
         mask = keep.tile([P, TOKENS], F32)
+        weight = keep.tile([P, TOKENS], F32)
         count = keep.tile([P, SAMPLES], F32)
 
         def by_sample(row):
             return row[:].rearrange("p (s t) -> p s t", t=SAMPLE_TOKENS)
 
         def make_mask():
-            mask_bank = psum.tile([P, TOKENS], F32, tag="bank%d" % HALF_TILES)
+            mask_bank = psum.tile([P, TOKENS], F32, tag="bank%d" % (OUT_TILES - 1))
             for h in range(TOKEN_TILES):
                 nc.tensor.matmul(
                     out=mask_bank[:, h * P : (h + 1) * P],
@@ -250,7 +260,28 @@ def tile_linearnnencoder_k_kernel(tc, x, W_words, W_scales, b, out):
                 ys.append((j, y))
             return ys
 
-        def statistics(ys):
+        negative = keep.tile([P, SAMPLES, OUT_TILES], F32)
+
+        def make_means():
+            factor = neg_inv_n[:].unsqueeze(2).to_broadcast([P, SAMPLES, OUT_TILES])
+            nc.vector.scalar_tensor_tensor(
+                out=means[:, 0], in0=neg_totals[:], scalar=0.0, in1=factor, op0=ALU.max, op1=ALU.mult
+            )
+            nc.vector.scalar_tensor_tensor(
+                out=negative[:], in0=neg_totals[:], scalar=0.0, in1=factor, op0=ALU.min, op1=ALU.mult
+            )
+            nc.vector.tensor_tensor(out=means[:, 1], in0=means[:, 0], in1=negative[:], op=ALU.add)
+            means_bank = psum.tile([P, P], F32, tag="bank2")
+            nc.tensor.transpose(means_bank[:], means[:].rearrange("p i s j -> p (i s j)"), ident[:])
+            return means_bank
+
+        def store_means(means_bank):
+            nc.vector.tensor_copy(out=final[half:P, :], in_=means_bank[half:P, :])
+            nc.sync.dma_start(
+                out=out[:, OUTPUTS : 2 * OUTPUTS].rearrange("s (j n) -> s j n", n=P), in_=final[half:P, :]
+            )
+
+        def statistics(ys, last=False):
             for j, y in ys:
                 nc.vector.tensor_tensor(out=y[:], in0=y[:], in1=mask[:], op=ALU.mult)
             for j, y in ys:
@@ -267,10 +298,16 @@ def tile_linearnnencoder_k_kernel(tc, x, W_words, W_scales, b, out):
                         scale=count[:, s : s + 1],
                         bias=neg_totals[:, s, j : j + 1],
                     )
+            if last:
+                means_bank = make_means()
             for j, y in ys:
-                nc.vector.tensor_tensor(out=y[:], in0=y[:], in1=mask[:], op=ALU.mult)
+                nc.vector.scalar_tensor_tensor(
+                    out=y[:], in0=y[:], scalar=0.0, in1=weight[:], op0=ALU.max, op1=ALU.mult
+                )
             for j, y in ys:
-                nc.vector.tensor_reduce(out=square_sums[:, :, j], in_=by_sample(y), axis=AXIS.X, op=ALU.add)
+                nc.vector.tensor_reduce(out=variances[:, 0, :, j], in_=by_sample(y), axis=AXIS.X, op=ALU.add)
+            if last:
+                store_means(means_bank)
 
         neg_inv_n = keep.tile([P, SAMPLES], F32)
         inv_var = keep.tile([P, SAMPLES], F32)
@@ -285,14 +322,21 @@ def tile_linearnnencoder_k_kernel(tc, x, W_words, W_scales, b, out):
             nc.vector.reciprocal(out=inv_var[:], in_=inv_var[:])
             nc.vector.reciprocal(out=neg_inv_n[:], in_=neg_inv_n[:])
             nc.vector.tensor_scalar_mul(out=neg_inv_n[:], in0=neg_inv_n[:], scalar1=-1.0)
+            nc.vector.tensor_tensor(
+                out=by_sample(weight),
+                in0=by_sample(mask),
+                in1=inv_var[:].unsqueeze(2).to_broadcast([P, SAMPLES, SAMPLE_TOKENS]),
+                op=ALU.mult,
+            )
 
+        open_groups(range(HALF_TILES, OUT_TILES - 1))
         for load in full_loads[:MASK_AFTER]:
-            multiply(load, range(load[1], load[1] + FULL_CHUNK), left)
+            multiply(load, range(load[1], load[1] + FULL_CHUNK), range(OUT_TILES - 1))
         make_mask()
         make_divisors()
-        open_groups(right)
+        open_groups([OUT_TILES - 1])
         for load in full_loads[:MASK_AFTER]:
-            multiply(load, range(load[1], load[1] + FULL_CHUNK), right)
+            multiply(load, range(load[1], load[1] + FULL_CHUNK), [OUT_TILES - 1])
         for first_pass in range(EARLY + FULL_CHUNK * len(full_loads), PASSES, FULL_CHUNK):
             full_loads.append(load_full(first_pass))
         late_loads = [
@@ -307,32 +351,13 @@ def tile_linearnnencoder_k_kernel(tc, x, W_words, W_scales, b, out):
             group = range(first_tile, first_tile + GROUP_TILES)
             for load in loads:
                 multiply(load, range(load[1], load[1] + LATE_CHUNK), group)
-            statistics(gelu(group))
+            statistics(gelu(group), last=first_tile + GROUP_TILES == OUT_TILES)
 
         nc.scalar.activation(out=warm[:], in_=warm[:], func=ACT.Sqrt)
 
-        def over_tiles(row):
-            return row[:].unsqueeze(2).to_broadcast([P, SAMPLES, OUT_TILES])
-
-        results = keep.tile([P, SAMPLES, 2, OUT_TILES], F32)
-        variance = keep.tile([P, SAMPLES, OUT_TILES], F32)
-        nc.vector.scalar_tensor_tensor(
-            out=variance[:],
-            in0=square_sums[:],
-            scalar=SMALLEST_SQUARE_SUM,
-            in1=over_tiles(inv_var),
-            op0=ALU.max,
-            op1=ALU.mult,
+        variances_bank = psum.tile([P, P], F32, tag="bank1")
+        nc.tensor.transpose(variances_bank[:], variances[:].rearrange("p i s j -> p (i s j)"), ident[:])
+        nc.scalar.activation(
+            out=final[0:half, :], in_=variances_bank[0:half, :], func=ACT.Sqrt, bias=tiny[0:half, :], scale=1.0
         )
-        nc.scalar.activation(out=results[:, :, 0, :], in_=variance[:], func=ACT.Sqrt)
-        nc.vector.tensor_tensor(out=results[:, :, 1, :], in0=neg_totals[:], in1=over_tiles(neg_inv_n), op=ALU.mult)
-
-        out_bank = psum.tile([P, P], F32, tag="bank1")
-        nc.tensor.transpose(out_bank[:], results[:].rearrange("p s i j -> p (s i j)"), ident[:])
-        positive = keep.tile([P, P], F32)
-        nc.vector.tensor_scalar_max(out=positive[:], in0=out_bank[:], scalar1=0.0)
-        final = keep.tile([P, P], F32)
-        nc.vector.scalar_tensor_tensor(
-            out=final[:], in0=out_bank[:], scalar=0.0, in1=positive[:], op0=ALU.min, op1=ALU.add
-        )
-        nc.sync.dma_start(out=out.rearrange("s (c n) -> (s c) n", n=P), in_=final[:])
+        nc.scalar.dma_start(out=out[:, 0:OUTPUTS].rearrange("s (j n) -> s j n", n=P), in_=final[0:half, :])

@@ -31,17 +31,16 @@ X_CHUNK = 4
 X_CHUNKS = PASSES // X_CHUNK
 RUN = 2
 RUNS = PASSES // RUN
-MX_LAG = 2
 PLANES = 4
-assert X_CHUNK == PLANES
 HALF_TILES = OUT_TILES // 2
-EARLY = 12
-FULL_CHUNK = 2
-MASK_AFTER = 6
-LEFT_STRIDE = 2
-LATE_CHUNK = 4
-GROUP_TILES = 2
-RING = 18
+EARLY_TILES = 6
+EARLY = 20
+SPLIT = 6
+W_CHUNK = 2
+SPLIT_CHUNK = 3
+LATE_CHUNKS = (8, 8, 4)
+assert sum(LATE_CHUNKS) == EARLY
+W_BUFS = 10
 PAD_WORD = -1.0058441162109375
 TINY = 2.0**-100
 
@@ -54,8 +53,8 @@ def tile_linearnnencoder_k_kernel(tc, x, W_words, W_scales, b, out):
         stack.enter_context(tc.manual_schedule())
         keep = stack.enter_context(tc.tile_pool(name="keep", bufs=1))
         stage = stack.enter_context(tc.tile_pool(name="stage", bufs=4))
-        ring = stack.enter_context(tc.tile_pool(name="ring", bufs=RING))
-        y_pool = stack.enter_context(tc.tile_pool(name="y_pool", bufs=HALF_TILES + GROUP_TILES))
+        w_pool = stack.enter_context(tc.tile_pool(name="w_pool", bufs=W_BUFS))
+        y_pool = stack.enter_context(tc.tile_pool(name="y_pool", bufs=EARLY_TILES))
         psum = stack.enter_context(tc.psum_pool(name="psum", bufs=1))
 
         ident = keep.tile([P, P], F32)
@@ -88,14 +87,14 @@ def tile_linearnnencoder_k_kernel(tc, x, W_words, W_scales, b, out):
                 acc[j] = psum.tile([P, TOKENS], F32, tag="bank%d" % j, name="acc%d" % j)
 
         def load_w(first_pass, passes, first_tile, tiles):
-            loaded = ring.tile([P, passes, tiles * P], U32, align_bytes=64, tag="load", name="w_load")
+            loaded = w_pool.tile([P, passes, tiles * P], U32, align_bytes=64, name="w_load")
             nc.sync.dma_start(
                 out=loaded[:].bitcast(I32),
                 in_=W_words[first_pass : first_pass + passes, :, first_tile * P : (first_tile + tiles) * P, :]
                 .rearrange("g p n t -> p g (n t)")
                 .bitcast(I32),
             )
-            return loaded, first_pass, first_tile
+            return loaded, range(first_pass, first_pass + passes), first_tile
 
         def load_scales(c):
             for quad in range(4):
@@ -104,50 +103,38 @@ def tile_linearnnencoder_k_kernel(tc, x, W_words, W_scales, b, out):
                     in_=W_scales[PLANES * c : PLANES * (c + 1), 4 * quad : 4 * quad + 4, :].bitcast(I32),
                 )
 
-        def multiply(load, passes, tiles):
-            loaded, first_pass, first_tile = load
+        def multiply(load, tiles):
+            loaded, passes, first_tile = load
             for g in passes:
                 for j in tiles:
                     cols = slice((j - first_tile) * P, (j - first_tile + 1) * P)
+                    first, last = (0, PASSES - 1) if j < EARLY_TILES else (EARLY, EARLY - 1)
                     nc.tensor.matmul_mx(
                         out=acc[j][:],
-                        lhsT=loaded[:, g - first_pass, cols].bitcast(FP8X4),
+                        lhsT=loaded[:, g - passes.start, cols].bitcast(FP8X4),
                         lhsT_scale=w_planes[4 * (g % PLANES) : P, g // PLANES, j * P : (j + 1) * P],
                         rhs=x_codes[:, g * TOKENS : (g + 1) * TOKENS].bitcast(FP8X4),
                         rhs_scale=x_scales[:, g * TOKENS : (g + 1) * TOKENS],
-                        start=(g == (0 if j < HALF_TILES else EARLY)),
-                        stop=(g == (PASSES if j < HALF_TILES else EARLY) - 1),
+                        start=(g == first),
+                        stop=(g == last),
                     )
-
-        left = range(HALF_TILES)
 
         x_view = x.flatten_outer_dims().rearrange("(h p) k -> p h k", p=P)
         x_cols = X_CHUNK * K_PASS
         x_tiles = []
-        left_loads = []
+        early_loads = []
 
-        def load_x(c):
-            x_tile = ring.tile([P, TOKEN_TILES, x_cols], BF16, align_bytes=64, tag="load", name="x_load")
-            nc.sync.dma_start(out=x_tile[:], in_=x_view[:, :, c * x_cols : (c + 1) * x_cols])
-            x_tiles.append(x_tile)
-
-        def load_left(c):
-            load_scales(c)
-            left_loads.append(load_w(c * PLANES, PLANES, 0, HALF_TILES))
-
-        def load_full(first_pass):
-            if first_pass % PLANES == 0:
-                load_scales(first_pass // PLANES)
-            return load_w(first_pass, FULL_CHUNK, 0, OUT_TILES)
+        def early_loads_behind(c):
+            return EARLY // W_CHUNK * c // (X_CHUNKS - 1)
 
         for c in range(X_CHUNKS):
-            load_x(c)
-            if c % LEFT_STRIDE == 0 and c // LEFT_STRIDE < EARLY // PLANES:
-                load_left(c // LEFT_STRIDE)
-        full_loads = [
-            load_full(first_pass)
-            for first_pass in range(EARLY, EARLY + FULL_CHUNK * (RING - X_CHUNKS - EARLY // PLANES), FULL_CHUNK)
-        ]
+            x_tile = keep.tile([P, TOKEN_TILES, x_cols], BF16, name="x%d" % c)
+            nc.sync.dma_start(out=x_tile[:], in_=x_view[:, :, c * x_cols : (c + 1) * x_cols])
+            x_tiles.append(x_tile)
+            for i in range(len(early_loads), early_loads_behind(c)):
+                if i * W_CHUNK % PLANES == 0:
+                    load_scales(i * W_CHUNK // PLANES)
+                early_loads.append(load_w(i * W_CHUNK, W_CHUNK, 0, EARLY_TILES))
 
         x_codes = keep.tile([P, PASSES * TOKENS], U32, align_bytes=64)
         x_scales = keep.tile([P, PASSES * TOKENS], U8, align_bytes=64)
@@ -162,7 +149,7 @@ def tile_linearnnencoder_k_kernel(tc, x, W_words, W_scales, b, out):
 
         def transpose_run(r, sorted_words, grouped):
             for i in range(RUN):
-                bank = psum.tile([P, 2, TOKENS], F32, tag="bank%d" % (HALF_TILES + (RUN * r + i) % HALF_TILES), name="x_bank")
+                bank = psum.tile([P, 2, TOKENS], F32, tag="bank%d" % (EARLY_TILES + i), name="x_bank")
                 for h in range(TOKEN_TILES):
                     for u in range(2):
                         nc.tensor.transpose(
@@ -180,9 +167,10 @@ def tile_linearnnencoder_k_kernel(tc, x, W_words, W_scales, b, out):
                 in_=grouped[:].rearrange("p g r t -> p (g r t)"),
             )
 
-        open_groups(left)
+        open_groups(range(EARLY_TILES))
         sorted_tiles = {0: sort_run(0)}
         grouped_tiles = {}
+        multiplied = 0
         for r in range(RUNS + 1):
             if r < RUNS:
                 grouped_tiles[r] = stage.tile([P, RUN, TOKENS, PACK], BF16, name="grouped", align_bytes=64)
@@ -191,9 +179,9 @@ def tile_linearnnencoder_k_kernel(tc, x, W_words, W_scales, b, out):
                 quantise_run(r - 1, grouped_tiles[r - 1])
             if r + 1 < RUNS:
                 sorted_tiles[r + 1] = sort_run(r + 1)
-            g = r - MX_LAG
-            if 0 <= g < EARLY:
-                multiply(left_loads[g // PLANES], [g], left)
+            if multiplied < early_loads_behind(r * RUN // X_CHUNK - 1):
+                multiply(early_loads[multiplied], range(EARLY_TILES))
+                multiplied += 1
 
         differs = keep.tile([P, X_CHUNKS], F32)
         distance = keep.tile([P, X_CHUNKS], F32)
@@ -329,29 +317,35 @@ def tile_linearnnencoder_k_kernel(tc, x, W_words, W_scales, b, out):
                 op=ALU.mult,
             )
 
-        open_groups(range(HALF_TILES, OUT_TILES - 1))
-        for load in full_loads[:MASK_AFTER]:
-            multiply(load, range(load[1], load[1] + FULL_CHUNK), range(OUT_TILES - 1))
+        left = range(HALF_TILES)
+        right = range(HALF_TILES, OUT_TILES)
+        for load in early_loads[multiplied:]:
+            multiply(load, range(EARLY_TILES))
+        open_groups(range(EARLY_TILES, OUT_TILES - 1))
+        full_loads = []
+        for first_pass in range(EARLY, PASSES - SPLIT, W_CHUNK):
+            if first_pass % PLANES == 0:
+                load_scales(first_pass // PLANES)
+            full_loads.append(load_w(first_pass, W_CHUNK, 0, OUT_TILES))
+            multiply(full_loads[-1], range(OUT_TILES - 1))
+        load_scales((PASSES - SPLIT) // PLANES + 1)
+        for first_pass in range(PASSES - SPLIT, PASSES, SPLIT_CHUNK):
+            multiply(load_w(first_pass, SPLIT_CHUNK, 0, HALF_TILES), left)
         make_mask()
         make_divisors()
         open_groups([OUT_TILES - 1])
-        for load in full_loads[:MASK_AFTER]:
-            multiply(load, range(load[1], load[1] + FULL_CHUNK), [OUT_TILES - 1])
-        for first_pass in range(EARLY + FULL_CHUNK * len(full_loads), PASSES, FULL_CHUNK):
-            full_loads.append(load_full(first_pass))
-        late_loads = [
-            (first_tile, [load_w(first_pass, LATE_CHUNK, first_tile, GROUP_TILES) for first_pass in range(0, EARLY, LATE_CHUNK)])
-            for first_tile in range(HALF_TILES, OUT_TILES, GROUP_TILES)
-        ]
-        for load in full_loads[MASK_AFTER:]:
-            multiply(load, range(load[1], load[1] + FULL_CHUNK), range(OUT_TILES))
-
+        for load in full_loads:
+            multiply(load, [OUT_TILES - 1])
         statistics(gelu(left))
-        for first_tile, loads in late_loads:
-            group = range(first_tile, first_tile + GROUP_TILES)
-            for load in loads:
-                multiply(load, range(load[1], load[1] + LATE_CHUNK), group)
-            statistics(gelu(group), last=first_tile + GROUP_TILES == OUT_TILES)
+        for first_pass in range(PASSES - SPLIT, PASSES, SPLIT_CHUNK):
+            multiply(load_w(first_pass, SPLIT_CHUNK, HALF_TILES, OUT_TILES - HALF_TILES), right)
+
+        statistics(gelu(range(HALF_TILES, EARLY_TILES)))
+        first_pass = 0
+        for passes in LATE_CHUNKS:
+            multiply(load_w(first_pass, passes, EARLY_TILES, OUT_TILES - EARLY_TILES), range(EARLY_TILES, OUT_TILES))
+            first_pass += passes
+        statistics(gelu(range(EARLY_TILES, OUT_TILES)), last=True)
 
         nc.scalar.activation(out=warm[:], in_=warm[:], func=ACT.Sqrt)
 

@@ -103,9 +103,9 @@ def tile_linearnnencoder_k_kernel(tc, x, W_words, W_scales, b, out):
                     in_=W_scales[PLANES * c : PLANES * (c + 1), 4 * quad : 4 * quad + 4, :].bitcast(I32),
                 )
 
-        def multiply(load, tiles):
+        def multiply(load, tiles, only=None):
             loaded, passes, first_tile = load
-            for g in passes:
+            for g in passes if only is None else [only]:
                 for j in tiles:
                     cols = slice((j - first_tile) * P, (j - first_tile + 1) * P)
                     first, last = (0, PASSES - 1) if j < EARLY_TILES else (EARLY, EARLY - 1)
@@ -125,7 +125,7 @@ def tile_linearnnencoder_k_kernel(tc, x, W_words, W_scales, b, out):
         early_loads = []
 
         def early_loads_behind(c):
-            return EARLY // W_CHUNK * c // (X_CHUNKS - 1)
+            return max(c, 0) if c + 1 < X_CHUNKS else EARLY // W_CHUNK
 
         for c in range(X_CHUNKS):
             x_tile = keep.tile([P, TOKEN_TILES, x_cols], BF16, name="x%d" % c)
@@ -167,6 +167,10 @@ def tile_linearnnencoder_k_kernel(tc, x, W_words, W_scales, b, out):
                 in_=grouped[:].rearrange("p g r t -> p (g r t)"),
             )
 
+        def multiply_early(first, end):
+            for g in range(first, end):
+                multiply(early_loads[g // W_CHUNK], range(EARLY_TILES), only=g)
+
         open_groups(range(EARLY_TILES))
         sorted_tiles = {0: sort_run(0)}
         grouped_tiles = {}
@@ -179,9 +183,11 @@ def tile_linearnnencoder_k_kernel(tc, x, W_words, W_scales, b, out):
                 quantise_run(r - 1, grouped_tiles[r - 1])
             if r + 1 < RUNS:
                 sorted_tiles[r + 1] = sort_run(r + 1)
-            if multiplied < early_loads_behind(r * RUN // X_CHUNK - 1):
-                multiply(early_loads[multiplied], range(EARLY_TILES))
-                multiplied += 1
+            c, run_of_chunk = divmod(r, X_CHUNK // RUN)
+            before, now = (W_CHUNK * early_loads_behind(c + d) for d in (-2, -1))
+            until = before + (now - before) * (run_of_chunk + 1) // (X_CHUNK // RUN)
+            multiply_early(multiplied, until)
+            multiplied = until
 
         differs = keep.tile([P, X_CHUNKS], F32)
         distance = keep.tile([P, X_CHUNKS], F32)
@@ -319,8 +325,7 @@ def tile_linearnnencoder_k_kernel(tc, x, W_words, W_scales, b, out):
 
         left = range(HALF_TILES)
         right = range(HALF_TILES, OUT_TILES)
-        for load in early_loads[multiplied:]:
-            multiply(load, range(EARLY_TILES))
+        multiply_early(multiplied, EARLY)
         open_groups(range(EARLY_TILES, OUT_TILES - 1))
         full_loads = []
         for first_pass in range(EARLY, PASSES - SPLIT, W_CHUNK):

@@ -38,8 +38,9 @@ EARLY = 20
 SPLIT = 6
 W_CHUNK = 2
 SPLIT_CHUNK = 3
-LATE_CHUNKS = (8, 8, 4)
-assert sum(LATE_CHUNKS) == EARLY
+LATE_CHUNKS = (8, 8)
+LAST_CHUNK = 4
+assert sum(LATE_CHUNKS) + LAST_CHUNK == EARLY
 W_BUFS = 10
 PAD_WORD = -1.0058441162109375
 TINY = 2.0**-100
@@ -224,6 +225,7 @@ def tile_linearnnencoder_k_kernel(tc, x, W_words, W_scales, b, out):
         variances = keep.tile([P, 2, SAMPLES, OUT_TILES], F32)
         nc.vector.memset(variances[:], 0.0)
         means = keep.tile([P, 2, SAMPLES, OUT_TILES], F32)
+        nc.vector.memset(means[:], 0.0)
         final = keep.tile([P, P], F32)
         half = SAMPLES * OUT_TILES
         mask = keep.tile([P, TOKENS], F32)
@@ -254,54 +256,56 @@ def tile_linearnnencoder_k_kernel(tc, x, W_words, W_scales, b, out):
                 ys.append((j, y))
             return ys
 
-        negative = keep.tile([P, SAMPLES, OUT_TILES], F32)
+        positive = keep.tile([P, P], F32)
 
         def make_means():
-            factor = neg_inv_n[:].unsqueeze(2).to_broadcast([P, SAMPLES, OUT_TILES])
-            nc.vector.scalar_tensor_tensor(
-                out=means[:, 0], in0=neg_totals[:], scalar=0.0, in1=factor, op0=ALU.max, op1=ALU.mult
+            nc.gpsimd.tensor_tensor(
+                out=means[:, 1],
+                in0=neg_totals[:],
+                in1=neg_inv_n[:].unsqueeze(2).to_broadcast([P, SAMPLES, OUT_TILES]),
+                op=ALU.mult,
             )
-            nc.vector.scalar_tensor_tensor(
-                out=negative[:], in0=neg_totals[:], scalar=0.0, in1=factor, op0=ALU.min, op1=ALU.mult
-            )
-            nc.vector.tensor_tensor(out=means[:, 1], in0=means[:, 0], in1=negative[:], op=ALU.add)
             means_bank = psum.tile([P, P], F32, tag="bank2")
             nc.tensor.transpose(means_bank[:], means[:].rearrange("p i s j -> p (i s j)"), ident[:])
             return means_bank
 
         def store_means(means_bank):
-            nc.vector.tensor_copy(out=final[half:P, :], in_=means_bank[half:P, :])
+            rows = slice(half, P)
+            nc.vector.tensor_scalar_max(out=positive[rows, :], in0=means_bank[rows, :], scalar1=0.0)
+            nc.vector.scalar_tensor_tensor(
+                out=final[rows, :], in0=means_bank[rows, :], scalar=0.0, in1=positive[rows, :], op0=ALU.min, op1=ALU.add
+            )
             nc.sync.dma_start(
                 out=out[:, OUTPUTS : 2 * OUTPUTS].rearrange("s (j n) -> s j n", n=P), in_=final[half:P, :]
             )
 
-        def statistics(ys, last=False):
-            for j, y in ys:
-                nc.vector.tensor_tensor(out=y[:], in0=y[:], in1=mask[:], op=ALU.mult)
-            for j, y in ys:
-                nc.vector.tensor_reduce(
-                    out=neg_totals[:, :, j], in_=by_sample(y), axis=AXIS.X, op=ALU.add, negate=True
+        def mask_y(j, y):
+            nc.vector.tensor_tensor(out=y[:], in0=y[:], in1=mask[:], op=ALU.mult)
+
+        def sum_y(j, y):
+            nc.vector.tensor_reduce(out=neg_totals[:, :, j], in_=by_sample(y), axis=AXIS.X, op=ALU.add, negate=True)
+
+        def square_y(j, y):
+            for s in range(SAMPLES):
+                tokens = slice(s * SAMPLE_TOKENS, (s + 1) * SAMPLE_TOKENS)
+                nc.scalar.activation(
+                    out=y[:, tokens],
+                    in_=y[:, tokens],
+                    func=ACT.Square,
+                    scale=count[:, s : s + 1],
+                    bias=neg_totals[:, s, j : j + 1],
                 )
-            for j, y in ys:
-                for s in range(SAMPLES):
-                    tokens = slice(s * SAMPLE_TOKENS, (s + 1) * SAMPLE_TOKENS)
-                    nc.scalar.activation(
-                        out=y[:, tokens],
-                        in_=y[:, tokens],
-                        func=ACT.Square,
-                        scale=count[:, s : s + 1],
-                        bias=neg_totals[:, s, j : j + 1],
-                    )
-            if last:
-                means_bank = make_means()
-            for j, y in ys:
-                nc.vector.scalar_tensor_tensor(
-                    out=y[:], in0=y[:], scalar=0.0, in1=weight[:], op0=ALU.max, op1=ALU.mult
-                )
-            for j, y in ys:
-                nc.vector.tensor_reduce(out=variances[:, 0, :, j], in_=by_sample(y), axis=AXIS.X, op=ALU.add)
-            if last:
-                store_means(means_bank)
+
+        def weigh_squares(j, y):
+            nc.vector.scalar_tensor_tensor(out=y[:], in0=y[:], scalar=0.0, in1=weight[:], op0=ALU.max, op1=ALU.mult)
+
+        def sum_squares(j, y):
+            nc.vector.tensor_reduce(out=variances[:, 0, :, j], in_=by_sample(y), axis=AXIS.X, op=ALU.add)
+
+        def statistics(ys):
+            for step in (mask_y, sum_y, square_y, weigh_squares, sum_squares):
+                for j, y in ys:
+                    step(j, y)
 
         neg_inv_n = keep.tile([P, SAMPLES], F32)
         inv_var = keep.tile([P, SAMPLES], F32)
@@ -350,7 +354,21 @@ def tile_linearnnencoder_k_kernel(tc, x, W_words, W_scales, b, out):
         for passes in LATE_CHUNKS:
             multiply(load_w(first_pass, passes, EARLY_TILES, OUT_TILES - EARLY_TILES), range(EARLY_TILES, OUT_TILES))
             first_pass += passes
-        statistics(gelu(range(EARLY_TILES, OUT_TILES)), last=True)
+        last_loads = [load_w(first_pass, LAST_CHUNK, j, 1) for j in range(EARLY_TILES, OUT_TILES)]
+        ys = []
+        for j, load in enumerate(last_loads, EARLY_TILES):
+            multiply(load, [j])
+            ys += gelu([j])
+            mask_y(*ys[-1])
+            sum_y(*ys[-1])
+        for j, y in ys:
+            square_y(j, y)
+        means_bank = make_means()
+        weigh_squares(*ys[0])
+        sum_squares(*ys[0])
+        weigh_squares(*ys[1])
+        sum_squares(*ys[1])
+        store_means(means_bank)
 
         nc.scalar.activation(out=warm[:], in_=warm[:], func=ACT.Sqrt)
 

@@ -34,11 +34,10 @@ RUNS = PASSES // RUN
 PLANES = 4
 HALF_TILES = OUT_TILES // 2
 EARLY_TILES = 6
-EARLY = 20
-SPLIT = 6
+EARLY = 24
 W_CHUNK = 2
-SPLIT_CHUNK = 3
-LATE_CHUNKS = (8, 8)
+HALF_CHUNK = 4
+LATE_CHUNKS = (8, 8, 4)
 LAST_CHUNK = 4
 assert sum(LATE_CHUNKS) + LAST_CHUNK == EARLY
 W_BUFS = 10
@@ -302,8 +301,13 @@ def tile_linearnnencoder_k_kernel(tc, x, W_words, W_scales, b, out):
         def sum_squares(j, y):
             nc.vector.tensor_reduce(out=variances[:, 0, :, j], in_=by_sample(y), axis=AXIS.X, op=ALU.add)
 
-        def statistics(ys):
-            for step in (mask_y, sum_y, square_y, weigh_squares, sum_squares):
+        def statistics(ys, meanwhile=None):
+            for step in (mask_y, sum_y, square_y):
+                for j, y in ys:
+                    step(j, y)
+            if meanwhile is not None:
+                meanwhile()
+            for step in (weigh_squares, sum_squares):
                 for j, y in ys:
                     step(j, y)
 
@@ -327,27 +331,17 @@ def tile_linearnnencoder_k_kernel(tc, x, W_words, W_scales, b, out):
                 op=ALU.mult,
             )
 
+        multiply_early(multiplied, EARLY)
         left = range(HALF_TILES)
         right = range(HALF_TILES, OUT_TILES)
-        multiply_early(multiplied, EARLY)
-        open_groups(range(EARLY_TILES, OUT_TILES - 1))
-        full_loads = []
-        for first_pass in range(EARLY, PASSES - SPLIT, W_CHUNK):
-            if first_pass % PLANES == 0:
-                load_scales(first_pass // PLANES)
-            full_loads.append(load_w(first_pass, W_CHUNK, 0, OUT_TILES))
-            multiply(full_loads[-1], range(OUT_TILES - 1))
-        load_scales((PASSES - SPLIT) // PLANES + 1)
-        for first_pass in range(PASSES - SPLIT, PASSES, SPLIT_CHUNK):
-            multiply(load_w(first_pass, SPLIT_CHUNK, 0, HALF_TILES), left)
+        for first_pass in range(EARLY, PASSES, HALF_CHUNK):
+            load_scales(first_pass // PLANES)
+            multiply(load_w(first_pass, HALF_CHUNK, 0, HALF_TILES), left)
         make_mask()
-        make_divisors()
-        open_groups([OUT_TILES - 1])
-        for load in full_loads:
-            multiply(load, [OUT_TILES - 1])
-        statistics(gelu(left))
-        for first_pass in range(PASSES - SPLIT, PASSES, SPLIT_CHUNK):
-            multiply(load_w(first_pass, SPLIT_CHUNK, HALF_TILES, OUT_TILES - HALF_TILES), right)
+        open_groups(range(EARLY_TILES, OUT_TILES))
+        statistics(gelu(left), meanwhile=make_divisors)
+        for first_pass in range(EARLY, PASSES, HALF_CHUNK):
+            multiply(load_w(first_pass, HALF_CHUNK, HALF_TILES, HALF_TILES), right)
 
         statistics(gelu(range(HALF_TILES, EARLY_TILES)))
         first_pass = 0

from contextlib import ExitStack

import concourse.mybir as mybir
from concourse.masks import make_identity

F32 = mybir.dt.float32
BF16 = mybir.dt.bfloat16
I32 = mybir.dt.int32
U32 = mybir.dt.uint32
U8 = mybir.dt.uint8
FP8X4 = mybir.dt.float8_e4m3fn_x4
ALU = mybir.AluOpType
ACT = mybir.ActivationFunctionType
AXIS = mybir.AxisListType

P = 128
PACK = 4
K_PASS = P * PACK
WORDS_PASS = K_PASS // 2

SAMPLES = 8
SAMPLE_TOKENS = 32
TOKENS = SAMPLES * SAMPLE_TOKENS
TOKEN_TILES = TOKENS // P
FEATURES = 16384
OUTPUTS = 1024
PASSES = FEATURES // K_PASS
OUT_TILES = OUTPUTS // P

X_CHUNK = 4
X_CHUNKS = PASSES // X_CHUNK
RUN = 2
RUNS = PASSES // RUN
PLANES = 4
HALF_TILES = OUT_TILES // 2
EARLY_TILES = 6
EARLY = 24
W_CHUNK = 2
HALF_CHUNK = 4
LATE_CHUNKS = (8, 8, 4)
LAST_CHUNK = 4
assert sum(LATE_CHUNKS) + LAST_CHUNK == EARLY
W_BUFS = 10
PAD_WORD = -1.0058441162109375
TINY = 2.0**-100

FLOPS = 2 * TOKENS * FEATURES * OUTPUTS


def tile_linearnnencoder_k_kernel(tc, x, W_words, W_scales, b, out):
    nc = tc.nc
    with ExitStack() as stack:
        stack.enter_context(tc.manual_schedule())
        keep = stack.enter_context(tc.tile_pool(name="keep", bufs=1))
        stage = stack.enter_context(tc.tile_pool(name="stage", bufs=4))
        w_pool = stack.enter_context(tc.tile_pool(name="w_pool", bufs=W_BUFS))
        y_pool = stack.enter_context(tc.tile_pool(name="y_pool", bufs=EARLY_TILES))
        psum = stack.enter_context(tc.psum_pool(name="psum", bufs=1))

        ident = keep.tile([P, P], F32)
        make_identity(nc, ident[:])

        w_planes = keep.tile([P, PASSES // PLANES, OUTPUTS], U8, align_bytes=64)
        nc.vector.memset(w_planes[:].bitcast(I32), 0)

        tiny = keep.tile([P, 1], F32)
        nc.vector.memset(tiny[:], TINY)

        warm = keep.tile([P, 1], F32)
        nc.vector.memset(warm[:], 1.0)
        nc.scalar.activation(out=warm[:], in_=warm[:], func=ACT.Gelu)

        b_rows = keep.tile([OUT_TILES, P], BF16)
        nc.sync.dma_start(out=b_rows[:], in_=b.rearrange("(j n) -> j n", n=P))
        b_square = keep.tile([P, P], F32)
        nc.vector.memset(b_square[:], 0.0)
        nc.vector.tensor_copy(out=b_square[0:OUT_TILES, :], in_=b_rows[:])
        b_bank = psum.tile([P, P], F32, tag="bank7")
        nc.tensor.transpose(b_bank[:], b_square[:], ident[:])
        b_col = keep.tile([P, OUT_TILES], F32)
        nc.vector.tensor_copy(out=b_col[:], in_=b_bank[:, 0:OUT_TILES])

        acc = {}

        def open_groups(tiles):
            for j in tiles:
                acc[j] = psum.tile([P, TOKENS], F32, tag="bank%d" % j, name="acc%d" % j)

        def load_w(first_pass, passes, first_tile, tiles):
            loaded = w_pool.tile([P, passes, tiles * P], U32, align_bytes=64, name="w_load")
            nc.sync.dma_start(
                out=loaded[:].bitcast(I32),
                in_=W_words[first_pass : first_pass + passes, :, first_tile * P : (first_tile + tiles) * P, :]
                .rearrange("g p n t -> p g (n t)")
                .bitcast(I32),
            )
            return loaded, range(first_pass, first_pass + passes), first_tile

        def load_scales(c):
            for quad in range(4):
                nc.sync.dma_start(
                    out=w_planes[32 * quad : 32 * quad + 4 * PLANES, c, :].bitcast(I32),
                    in_=W_scales[PLANES * c : PLANES * (c + 1), 4 * quad : 4 * quad + 4, :].bitcast(I32),
                )

        def multiply(load, tiles, only=None):
            loaded, passes, first_tile = load
            for g in passes if only is None else [only]:
                for j in tiles:
                    cols = slice((j - first_tile) * P, (j - first_tile + 1) * P)
                    first, last = (0, PASSES - 1) if j < EARLY_TILES else (EARLY, EARLY - 1)
                    nc.tensor.matmul_mx(
                        out=acc[j][:],
                        lhsT=loaded[:, g - passes.start, cols].bitcast(FP8X4),
                        lhsT_scale=w_planes[4 * (g % PLANES) : P, g // PLANES, j * P : (j + 1) * P],
                        rhs=x_codes[:, g * TOKENS : (g + 1) * TOKENS].bitcast(FP8X4),
                        rhs_scale=x_scales[:, g * TOKENS : (g + 1) * TOKENS],
                        start=(g == first),
                        stop=(g == last),
                    )

        x_view = x.flatten_outer_dims().rearrange("(h p) k -> p h k", p=P)
        x_cols = X_CHUNK * K_PASS
        x_tiles = []
        early_loads = []

        def early_loads_behind(c):
            return max(c, 0) if c + 1 < X_CHUNKS else EARLY // W_CHUNK

        for c in range(X_CHUNKS):
            x_tile = keep.tile([P, TOKEN_TILES, x_cols], BF16, name="x%d" % c)
            nc.sync.dma_start(out=x_tile[:], in_=x_view[:, :, c * x_cols : (c + 1) * x_cols])
            x_tiles.append(x_tile)
            for i in range(len(early_loads), early_loads_behind(c)):
                if i * W_CHUNK % PLANES == 0:
                    load_scales(i * W_CHUNK // PLANES)
                early_loads.append(load_w(i * W_CHUNK, W_CHUNK, 0, EARLY_TILES))

        x_codes = keep.tile([P, PASSES * TOKENS], U32, align_bytes=64)
        x_scales = keep.tile([P, PASSES * TOKENS], U8, align_bytes=64)

        def sort_run(r):
            sorted_words = stage.tile([P, TOKEN_TILES, 2, RUN * P], F32, name="sorted_words", align_bytes=64)
            first_word = (r * RUN % X_CHUNK) * WORDS_PASS
            words = x_tiles[r * RUN // X_CHUNK][:].rearrange("p h k -> p (h k)").bitcast(F32)
            words = words.rearrange("p (h k) -> p h k", h=TOKEN_TILES)[:, :, first_word : first_word + RUN * WORDS_PASS]
            nc.vector.tensor_copy(out=sorted_words[:], in_=words.rearrange("p h (w u) -> p h u w", u=2))
            return sorted_words

        def transpose_run(r, sorted_words, grouped):
            for i in range(RUN):
                bank = psum.tile([P, 2, TOKENS], F32, tag="bank%d" % (EARLY_TILES + i), name="x_bank")
                for h in range(TOKEN_TILES):
                    for u in range(2):
                        nc.tensor.transpose(
                            bank[:, u, h * P : (h + 1) * P],
                            sorted_words[:, h, u, i * P : (i + 1) * P],
                            ident[:],
                        )
                nc.scalar.copy(out=grouped[:, i].bitcast(F32), in_=bank[:].rearrange("p u r -> p r u"))

        def quantise_run(r, grouped):
            cols = slice(r * RUN * TOKENS, (r + 1) * RUN * TOKENS)
            nc.vector.quantize_mx(
                out=x_codes[:, cols].bitcast(FP8X4),
                scales=x_scales[:, cols],
                in_=grouped[:].rearrange("p g r t -> p (g r t)"),
            )

        def multiply_early(first, end):
            for g in range(first, end):
                multiply(early_loads[g // W_CHUNK], range(EARLY_TILES), only=g)

        open_groups(range(EARLY_TILES))
        sorted_tiles = {0: sort_run(0)}
        grouped_tiles = {}
        multiplied = 0
        for r in range(RUNS + 1):
            if r < RUNS:
                grouped_tiles[r] = stage.tile([P, RUN, TOKENS, PACK], BF16, name="grouped", align_bytes=64)
                transpose_run(r, sorted_tiles[r], grouped_tiles[r])
            if r >= 1:
                quantise_run(r - 1, grouped_tiles[r - 1])
            if r + 1 < RUNS:
                sorted_tiles[r + 1] = sort_run(r + 1)
            c, run_of_chunk = divmod(r, X_CHUNK // RUN)
            before, now = (W_CHUNK * early_loads_behind(c + d) for d in (-2, -1))
            until = before + (now - before) * (run_of_chunk + 1) // (X_CHUNK // RUN)
            multiply_early(multiplied, until)
            multiplied = until

        differs = keep.tile([P, X_CHUNKS], F32)
        distance = keep.tile([P, X_CHUNKS], F32)
        minus_pad = keep.tile([P, 1], F32)
        nc.vector.memset(minus_pad[:], -PAD_WORD)
        for c in range(X_CHUNKS):
            vector_words = x_tiles[c][:, 0, :].bitcast(F32)
            scalar_words = x_tiles[c][:, 1, :].bitcast(F32)
            nc.vector.tensor_scalar(
                out=vector_words,
                in0=vector_words,
                scalar1=PAD_WORD,
                scalar2=None,
                op0=ALU.not_equal,
                op1=ALU.max,
                accum_out=differs[:, c : c + 1],
            )
            nc.scalar.activation(
                out=scalar_words,
                in_=scalar_words,
                func=ACT.Square,
                bias=minus_pad[:],
                scale=1.0,
                accum_out=distance[:, c : c + 1],
            )

        valid = keep.tile([P, TOKEN_TILES], F32)
        row_distance = keep.tile([P, 1], F32)
        nc.vector.tensor_reduce(out=valid[:, 0:1], in_=differs[:], axis=AXIS.X, op=ALU.max)
        nc.vector.tensor_reduce(out=row_distance[:], in_=distance[:], axis=AXIS.X, op=ALU.add)
        nc.vector.tensor_single_scalar(out=valid[:, 1:2], in_=row_distance[:], scalar=0.0, op=ALU.not_equal)

        neg_totals = keep.tile([P, SAMPLES, OUT_TILES], F32)
        variances = keep.tile([P, 2, SAMPLES, OUT_TILES], F32)
        nc.vector.memset(variances[:], 0.0)
        means = keep.tile([P, 2, SAMPLES, OUT_TILES], F32)
        nc.vector.memset(means[:], 0.0)
        final = keep.tile([P, P], F32)
        half = SAMPLES * OUT_TILES
        mask = keep.tile([P, TOKENS], F32)
        weight = keep.tile([P, TOKENS], F32)
        count = keep.tile([P, SAMPLES], F32)

        def by_sample(row):
            return row[:].rearrange("p (s t) -> p s t", t=SAMPLE_TOKENS)

        def make_mask():
            mask_bank = psum.tile([P, TOKENS], F32, tag="bank%d" % (OUT_TILES - 1))
            for h in range(TOKEN_TILES):
                nc.tensor.matmul(
                    out=mask_bank[:, h * P : (h + 1) * P],
                    lhsT=valid[:, h : h + 1].to_broadcast([P, P]),
                    rhs=ident[:],
                    start=True,
                    stop=True,
                )
            nc.vector.tensor_copy(out=mask[:], in_=mask_bank[:])
            nc.vector.tensor_reduce(out=count[:], in_=by_sample(mask), axis=AXIS.X, op=ALU.add)

        def gelu(group):
            ys = []
            for j in group:
                y = y_pool.tile([P, TOKENS], F32)
                nc.scalar.activation(out=y[:], in_=acc[j][:], func=ACT.Gelu, bias=b_col[:, j : j + 1], scale=1.0)
                ys.append((j, y))
            return ys

        positive = keep.tile([P, P], F32)

        def make_means():
            nc.gpsimd.tensor_tensor(
                out=means[:, 1],
                in0=neg_totals[:],
                in1=neg_inv_n[:].unsqueeze(2).to_broadcast([P, SAMPLES, OUT_TILES]),
                op=ALU.mult,
            )
            means_bank = psum.tile([P, P], F32, tag="bank2")
            nc.tensor.transpose(means_bank[:], means[:].rearrange("p i s j -> p (i s j)"), ident[:])
            return means_bank

        def store_means(means_bank):
            rows = slice(half, P)
            nc.vector.tensor_scalar_max(out=positive[rows, :], in0=means_bank[rows, :], scalar1=0.0)
            nc.vector.scalar_tensor_tensor(
                out=final[rows, :], in0=means_bank[rows, :], scalar=0.0, in1=positive[rows, :], op0=ALU.min, op1=ALU.add
            )
            nc.sync.dma_start(
                out=out[:, OUTPUTS : 2 * OUTPUTS].rearrange("s (j n) -> s j n", n=P), in_=final[half:P, :]
            )

        def mask_y(j, y):
            nc.vector.tensor_tensor(out=y[:], in0=y[:], in1=mask[:], op=ALU.mult)

        def sum_y(j, y):
            nc.vector.tensor_reduce(out=neg_totals[:, :, j], in_=by_sample(y), axis=AXIS.X, op=ALU.add, negate=True)

        def square_y(j, y):
            for s in range(SAMPLES):
                tokens = slice(s * SAMPLE_TOKENS, (s + 1) * SAMPLE_TOKENS)
                nc.scalar.activation(
                    out=y[:, tokens],
                    in_=y[:, tokens],
                    func=ACT.Square,
                    scale=count[:, s : s + 1],
                    bias=neg_totals[:, s, j : j + 1],
                )

        def weigh_squares(j, y):
            nc.vector.scalar_tensor_tensor(out=y[:], in0=y[:], scalar=0.0, in1=weight[:], op0=ALU.max, op1=ALU.mult)

        def sum_squares(j, y):
            nc.vector.tensor_reduce(out=variances[:, 0, :, j], in_=by_sample(y), axis=AXIS.X, op=ALU.add)

        def statistics(ys, meanwhile=None):
            for step in (mask_y, sum_y, square_y):
                for j, y in ys:
                    step(j, y)
            if meanwhile is not None:
                meanwhile()
            for step in (weigh_squares, sum_squares):
                for j, y in ys:
                    step(j, y)

        neg_inv_n = keep.tile([P, SAMPLES], F32)
        inv_var = keep.tile([P, SAMPLES], F32)

        def make_divisors():
            nc.vector.tensor_scalar_max(out=neg_inv_n[:], in0=count[:], scalar1=1.0)
            nc.vector.tensor_scalar(
                out=inv_var[:], in0=count[:], scalar1=-1.0, scalar2=1.0, op0=ALU.add, op1=ALU.max
            )
            nc.vector.tensor_tensor(out=inv_var[:], in0=inv_var[:], in1=neg_inv_n[:], op=ALU.mult)
            nc.vector.tensor_tensor(out=inv_var[:], in0=inv_var[:], in1=neg_inv_n[:], op=ALU.mult)
            nc.vector.reciprocal(out=inv_var[:], in_=inv_var[:])
            nc.vector.reciprocal(out=neg_inv_n[:], in_=neg_inv_n[:])
            nc.vector.tensor_scalar_mul(out=neg_inv_n[:], in0=neg_inv_n[:], scalar1=-1.0)
            nc.vector.tensor_tensor(
                out=by_sample(weight),
                in0=by_sample(mask),
                in1=inv_var[:].unsqueeze(2).to_broadcast([P, SAMPLES, SAMPLE_TOKENS]),
                op=ALU.mult,
            )

        multiply_early(multiplied, EARLY)
        left = range(HALF_TILES)
        right = range(HALF_TILES, OUT_TILES)
        for first_pass in range(EARLY, PASSES, HALF_CHUNK):
            load_scales(first_pass // PLANES)
            multiply(load_w(first_pass, HALF_CHUNK, 0, HALF_TILES), left)
        make_mask()
        open_groups(range(EARLY_TILES, OUT_TILES))
        statistics(gelu(left), meanwhile=make_divisors)
        for first_pass in range(EARLY, PASSES, HALF_CHUNK):
            multiply(load_w(first_pass, HALF_CHUNK, HALF_TILES, HALF_TILES), right)

        statistics(gelu(range(HALF_TILES, EARLY_TILES)))
        first_pass = 0
        for passes in LATE_CHUNKS:
            multiply(load_w(first_pass, passes, EARLY_TILES, OUT_TILES - EARLY_TILES), range(EARLY_TILES, OUT_TILES))
            first_pass += passes
        last_loads = [load_w(first_pass, LAST_CHUNK, j, 1) for j in range(EARLY_TILES, OUT_TILES)]
        ys = []
        for j, load in enumerate(last_loads, EARLY_TILES):
            multiply(load, [j])
            ys += gelu([j])
            mask_y(*ys[-1])
            sum_y(*ys[-1])
        for j, y in ys:
            square_y(j, y)
        means_bank = make_means()
        weigh_squares(*ys[0])
        sum_squares(*ys[0])
        weigh_squares(*ys[1])
        sum_squares(*ys[1])
        store_means(means_bank)

        nc.scalar.activation(out=warm[:], in_=warm[:], func=ACT.Sqrt)

        variances_bank = psum.tile([P, P], F32, tag="bank1")
        nc.tensor.transpose(variances_bank[:], variances[:].rearrange("p i s j -> p (i s j)"), ident[:])
        nc.scalar.activation(
            out=final[0:half, :], in_=variances_bank[0:half, :], func=ACT.Sqrt, bias=tiny[0:half, :], scale=1.0
        )
        nc.scalar.dma_start(out=out[:, 0:OUTPUTS].rearrange("s (j n) -> s j n", n=P), in_=final[0:half, :])
